import numpy as np
import ml_dtypes


def mxq(x, axis, fmt="e4m3"):
    dtype, down = {"e4m3": (ml_dtypes.float8_e4m3fn, 7), "e5m2": (ml_dtypes.float8_e5m2, 14)}[fmt]
    v = np.moveaxis(np.asarray(x, np.float32).astype(ml_dtypes.bfloat16).astype(np.float64), axis, -1)
    blocks = v.reshape(v.shape[:-1] + (-1, 32))
    amax = np.abs(blocks).max(-1, keepdims=True)
    byte = np.maximum(np.where(amax > 0, np.frexp(amax)[1] - 1 + 127, 0) - down, 1)
    scale = np.exp2(byte - 127.0)
    codes = (blocks / scale).astype(np.float32).astype(dtype).astype(np.float64)
    return np.moveaxis((codes * scale).reshape(v.shape), -1, axis)


WIDE = False


def mx_kscale(k):
    if not WIDE:
        return np.ones(k)
    levels = np.array([10, -10, 5, -5, 0])
    a = np.random.permutation(np.resize(levels, k // 512 * 4)).reshape(k // 512, 4)
    idx = np.arange(k)
    return np.exp2(a[idx // 512, idx % 128 // 32])


BF16 = ml_dtypes.bfloat16


def bf(x):
    return np.asarray(x, np.float32).astype(BF16)


def f64(x):
    return np.asarray(x).astype(np.float64)


E2M1 = np.array([0.0, 0.5, 1.0, 1.5, 2.0, 3.0, 4.0, 6.0, -0.0, -0.5, -1.0, -1.5, -2.0, -3.0, -4.0, -6.0])


def pack_weight(w, fmt):
    k, n = w.shape
    w = f64(bf(w)).reshape(k // 32, 32, n)
    amax = np.abs(w).max(1)
    if fmt == "e4m3":
        byte = np.frexp(amax)[1] - 1 + 127 - 7
    else:
        mant, ex = np.frexp(amax / 6.0)
        byte = np.where(mant > 0.5, ex, ex - 1) + 127
    byte = np.clip(np.where(amax > 0, byte, 1), 1, 254)
    scaled = (w * np.exp2(127.0 - byte)[:, None, :]).reshape(k, n).astype(np.float32)
    by_word = np.ascontiguousarray(scaled.reshape(k // 512, 128, 4, n).transpose(0, 1, 3, 2))
    if fmt == "e4m3":
        words = by_word.astype(ml_dtypes.float8_e4m3fn).view(np.uint8)
    else:
        c = by_word.astype(ml_dtypes.float4_e2m1fn).view(np.uint8) & 0xF
        words = c[..., 0::2] | (c[..., 1::2] << 4)
    return np.ascontiguousarray(words), np.ascontiguousarray(byte.astype(np.uint8).reshape(k // 512, 16, n))


def unpack_weight(words, scales, fmt):
    g, p, n, _ = words.shape
    if fmt == "e4m3":
        vals = np.ascontiguousarray(words).view(ml_dtypes.float8_e4m3fn).astype(np.float64)
    else:
        nib = np.empty((g, p, n, 4), np.uint8)
        nib[..., 0::2] = words & 0xF
        nib[..., 1::2] = words >> 4
        vals = E2M1[nib]
    vals = vals * np.repeat(np.exp2(scales.astype(np.float64) - 127.0), 8, axis=1)[..., None]
    return vals.transpose(0, 1, 3, 2).reshape(g * 512, n)


L, B, D, F, TC = 8, 4096, 512, 1024, 4
EPS = 1e-5
NT = 100
ERF_C = 1.0 / np.cumprod(2.0 * np.arange(NT) + 1.0)


def erf(v):
    a = np.minimum(np.abs(v), 6.0)
    q = 2.0 * a * a
    acc = np.full_like(q, ERF_C[-1])
    for c in ERF_C[-2::-1]:
        acc = acc * q + c
    return np.sign(v) * (2.0 / np.sqrt(np.pi)) * a * np.exp(-a * a) * acc


def gelu(v):
    return 0.5 * v * (1.0 + erf(v / np.sqrt(2.0)))


def layer_norm(x, g, b):
    m = x.mean(-1, keepdims=True)
    v = ((x - m) ** 2).mean(-1, keepdims=True)
    return (x - m) / np.sqrt(v + EPS) * g + b


def setup_inputs():
    s, t = mx_kscale(D), mx_kscale(F)
    z = bf(np.random.standard_normal((B, D)) * s)
    W1_words, W1_scales = pack_weight(np.random.standard_normal((D, F)) / np.sqrt(D) / s[:, None], "e4m3")
    b1 = bf(np.random.standard_normal(F) * 0.3)
    g1 = bf((1.0 + 0.1 * np.random.standard_normal(F)) * t)
    be1 = bf(0.1 * np.random.standard_normal(F) * t)
    W2_words, W2_scales = pack_weight(np.random.standard_normal((F, D)) / np.sqrt(F) / t[:, None], "e4m3")
    b2 = bf(np.random.standard_normal(D) * 0.3)
    g2 = bf(1.0 + 0.1 * np.random.standard_normal(D))
    be2 = bf(0.1 * np.random.standard_normal(D))
    return {"z": z,
            "W1_words": W1_words,
            "W1_scales": W1_scales,
            "b1": b1,
            "g1": g1,
            "be1": be1,
            "W2_words": W2_words,
            "W2_scales": W2_scales,
            "b2": b2,
            "g2": g2,
            "be2": be2}


def reference(z, W1_words, W1_scales, b1, g1, be1, W2_words, W2_scales, b2, g2, be2):
    h = gelu((mxq(f64(z), 1, "e4m3") @ unpack_weight(W1_words, W1_scales, "e4m3")) + f64(b1))
    h = layer_norm(h, f64(g1), f64(be1))
    return layer_norm((mxq(h, 1, "e4m3") @ unpack_weight(W2_words, W2_scales, "e4m3")) + f64(b2), f64(g2), f64(be2))

@@ -1,0 +1,308 @@
+from contextlib import ExitStack
+
+import concourse.mybir as mybir
+from concourse.masks import make_identity
+
+FLOPS = 2 * 4096 * 512 * 1024 * 2
+
+F32 = mybir.dt.float32
+BF16 = mybir.dt.bfloat16
+I32 = mybir.dt.int32
+U32 = mybir.dt.uint32
+U8 = mybir.dt.uint8
+FP8X4 = mybir.dt.float8_e4m3fn_x4
+ALU = mybir.AluOpType
+ACT = mybir.ActivationFunctionType
+
+P = 128
+PACK = 4
+K_PASS = P * PACK
+ROWS = 4096
+D = 512
+F = 1024
+F_PASSES = F // K_PASS
+ROW_TILES = ROWS // P
+Z_CHUNK = 4
+EPS = 1e-5
+
+
+def tile_emaaggregator_pa_t_kernel(
+    tc, z, W1_words, W1_scales, b1, g1, be1, W2_words, W2_scales, b2, g2, be2, out
+):
+    nc = tc.nc
+    with ExitStack() as ctx:
+        consts = ctx.enter_context(tc.tile_pool(name="consts", bufs=1))
+        zq_pool = ctx.enter_context(tc.tile_pool(name="zq", bufs=3))
+        wide = ctx.enter_context(tc.tile_pool(name="wide", bufs=4))
+        hq_pool = ctx.enter_context(tc.tile_pool(name="hq", bufs=3))
+        outs = ctx.enter_context(tc.tile_pool(name="outs", bufs=4))
+        stats = ctx.enter_context(tc.tile_pool(name="stats", bufs=6))
+        psum_z = ctx.enter_context(tc.psum_pool(name="psum_z", bufs=1))
+        psum_s1 = ctx.enter_context(tc.psum_pool(name="psum_s1", bufs=3))
+        psum_ht = ctx.enter_context(tc.psum_pool(name="psum_ht", bufs=2))
+        psum_y = ctx.enter_context(tc.psum_pool(name="psum_y", bufs=2))
+
+        z_rows = z.rearrange("(p i) k -> p i k", i=ROW_TILES)
+        out_rows = out.rearrange("(p i) d -> p i d", i=ROW_TILES)
+
+        w1_scales = consts.tile([P, F], U8, align_bytes=64)
+        w2_scales = consts.tile([P, F_PASSES, D], U8, align_bytes=64)
+        nc.vector.memset(w1_scales[:].bitcast(I32), 0)
+        nc.vector.memset(w2_scales[:].bitcast(I32), 0)
+        neg_half = consts.tile([P, 1], F32)
+        nc.vector.memset(neg_half[:], -0.5)
+        ident = consts.tile([P, P], F32)
+        make_identity(nc, ident[:])
+
+        z_sb = consts.tile([P, ROW_TILES, D], BF16)
+        nc.sync.dma_start(out=z_sb[:, 0:Z_CHUNK, :], in_=z_rows[:, 0:Z_CHUNK, :])
+        w1_words = consts.tile([P, F], U32, align_bytes=64)
+        nc.sync.dma_start(
+            out=w1_words[:].bitcast(I32),
+            in_=W1_words[0].rearrange("p n t -> p (n t)").bitcast(I32),
+        )
+        for q in range(4):
+            nc.sync.dma_start(
+                out=w1_scales[32 * q : 32 * q + 4, :].bitcast(I32),
+                in_=W1_scales[0, 4 * q : 4 * q + 4, :].bitcast(I32),
+            )
+        w2_words = consts.tile([P, F_PASSES, D], U32, align_bytes=64)
+        for g in range(F_PASSES):
+            nc.sync.dma_start(
+                out=w2_words[:, g, :].bitcast(I32),
+                in_=W2_words[g].rearrange("p n t -> p (n t)").bitcast(I32),
+            )
+            for q in range(4):
+                nc.sync.dma_start(
+                    out=w2_scales[32 * q : 32 * q + 4, g, :].bitcast(I32),
+                    in_=W2_scales[g, 4 * q : 4 * q + 4, :].bitcast(I32),
+                )
+        for c in range(1, ROW_TILES // Z_CHUNK):
+            rows = slice(c * Z_CHUNK, (c + 1) * Z_CHUNK)
+            nc.sync.dma_start(out=z_sb[:, rows, :], in_=z_rows[:, rows, :])
+
+        b1_bc = consts.tile([P, F], BF16)
+        nc.scalar.dma_start(out=b1_bc[:], in_=b1.partition_broadcast(P))
+        g1_raw = consts.tile([P, F_PASSES, PACK], BF16)
+        nc.scalar.dma_start(out=g1_raw[:], in_=g1.rearrange("(g p t) -> p g t", g=F_PASSES, t=PACK))
+        be1_raw = consts.tile([P, F_PASSES, PACK], BF16)
+        nc.scalar.dma_start(out=be1_raw[:], in_=be1.rearrange("(g p t) -> p g t", g=F_PASSES, t=PACK))
+        b2_bc = consts.tile([P, D], BF16)
+        nc.scalar.dma_start(out=b2_bc[:], in_=b2.partition_broadcast(P))
+        g2_bc = consts.tile([P, D], BF16)
+        nc.scalar.dma_start(out=g2_bc[:], in_=g2.partition_broadcast(P))
+        be2_bc = consts.tile([P, D], BF16)
+        nc.scalar.dma_start(out=be2_bc[:], in_=be2.partition_broadcast(P))
+        b1_gtp = consts.tile([P, F_PASSES, PACK, P], BF16)
+        nc.vector.tensor_copy(
+            out=b1_gtp[:], in_=b1_bc[:].rearrange("r (g p t) -> r g t p", g=F_PASSES, t=PACK)
+        )
+        g1_col = consts.tile([P, F_PASSES * PACK], F32)
+        nc.vector.tensor_copy(out=g1_col[:], in_=g1_raw[:].rearrange("p g t -> p (g t)"))
+        be1_col = consts.tile([P, F_PASSES * PACK], F32)
+        nc.vector.tensor_copy(out=be1_col[:], in_=be1_raw[:].rearrange("p g t -> p (g t)"))
+
+        junk = consts.tile([P, F], BF16)
+
+        zt_of, zg_of, zq_of, acc1_of, x_of, mean1_of, sq1_of, n_of = {}, {}, {}, {}, {}, {}, {}, {}
+        ht_of, planes_of, hg_of, hq_of, acc2_of, y_of, mean2_of, sq2_of, rstd2_of, scaled_of = (
+            {}, {}, {}, {}, {}, {}, {}, {}, {}, {},
+        )
+
+        def flat(tile4):
+            return tile4[:].rearrange("r g t p -> r (g t p)")
+
+        def transpose_z(i):
+            zt = psum_z.tile([P, 2, P], F32)
+            words = z_sb[:, i, :].bitcast(F32)
+            for u in range(2):
+                nc.tensor.transpose(zt[:, u, :], words[:, u : D // 2 : 2], ident[:])
+            zt_of[i] = zt
+
+        def group_z(i):
+            z_grouped = zq_pool.tile([P, P, 2], F32, align_bytes=64)
+            nc.vector.tensor_copy(out=z_grouped[:], in_=zt_of[i][:].rearrange("p u r -> p r u"))
+            zg_of[i] = z_grouped
+
+        def quantise_z(i):
+            z_words = zq_pool.tile([P, P], U32, align_bytes=64)
+            z_scales = zq_pool.tile([P, P], U8, align_bytes=64)
+            nc.vector.quantize_mx(
+                out=z_words[:].bitcast(FP8X4),
+                scales=z_scales[:],
+                in_=zg_of[i][:].rearrange("p r u -> p (r u)").bitcast(BF16),
+            )
+            zq_of[i] = (z_words, z_scales)
+
+        def matmul_1(i):
+            z_words, z_scales = zq_of[i]
+            acc1_of[i] = []
+            for g in range(F_PASSES):
+                acc = psum_s1.tile([P, K_PASS], F32)
+                nc.tensor.matmul_mx(
+                    out=acc[:],
+                    lhsT=z_words[:].bitcast(FP8X4),
+                    lhsT_scale=z_scales[:],
+                    rhs=w1_words[:, g * K_PASS : (g + 1) * K_PASS].bitcast(FP8X4),
+                    rhs_scale=w1_scales[:, g * K_PASS : (g + 1) * K_PASS],
+                    start=True,
+                    stop=True,
+                )
+                acc1_of[i].append(acc)
+
+        def add_b1(i):
+            x = wide.tile([P, F_PASSES, PACK, P], F32)
+            for g in range(F_PASSES):
+                nc.vector.tensor_tensor(
+                    out=x[:, g],
+                    in0=acc1_of[i][g][:].rearrange("r (p t) -> r t p", t=PACK),
+                    in1=b1_gtp[:, g],
+                    op=ALU.add,
+                )
+            x_of[i] = x
+
+        def gelu_and_moments(i):
+            x_flat = flat(x_of[i])
+            sum_x = stats.tile([P, 1], F32)
+            nc.scalar.activation(out=x_flat, in_=x_flat, func=ACT.Gelu, accum_out=sum_x[:])
+            neg_mean = stats.tile([P, 1], F32)
+            nc.scalar.mul(out=neg_mean[:], in_=sum_x[:], mul=-1.0 / F)
+            sum_sq = stats.tile([P, 1], F32)
+            nc.scalar.activation(out=junk[:], in_=x_flat, func=ACT.Square, bias=neg_mean[:], accum_out=sum_sq[:])
+            mean1_of[i] = neg_mean
+            sq1_of[i] = sum_sq
+
+        def inv_std(sum_sq, width):
+            var = stats.tile([P, 1], F32)
+            nc.gpsimd.tensor_scalar(
+                out=var[:], in0=sum_sq[:], scalar1=1.0 / width, scalar2=EPS, op0=ALU.mult, op1=ALU.add
+            )
+            rstd = stats.tile([P, 1], F32)
+            nc.gpsimd.tensor_tensor(out=rstd[:], in0=var[:], in1=neg_half[:], op=ALU.pow)
+            return rstd
+
+        def normalise_1(i):
+            rstd = inv_std(sq1_of[i], F)
+            n = wide.tile([P, F_PASSES, PACK, P], F32)
+            nc.gpsimd.tensor_scalar(
+                out=flat(n),
+                in0=flat(x_of[i]),
+                scalar1=mean1_of[i][:],
+                scalar2=rstd[:],
+                op0=ALU.add,
+                op1=ALU.mult,
+            )
+            n_of[i] = n
+
+        def transpose_n(i):
+            ht_of[i] = []
+            for g in range(F_PASSES):
+                ht = psum_ht.tile([P, PACK, P], F32)
+                for t in range(PACK):
+                    nc.tensor.transpose(ht[:, t, :], n_of[i][:, g, t, :], ident[:])
+                ht_of[i].append(ht)
+
+        def scale_shift_1(i):
+            planes = hq_pool.tile([P, F_PASSES, PACK, P], BF16)
+            for g in range(F_PASSES):
+                for t in range(PACK):
+                    col = g * PACK + t
+                    nc.scalar.activation(
+                        out=planes[:, g, t, :],
+                        in_=ht_of[i][g][:, t, :],
+                        func=ACT.Identity,
+                        scale=g1_col[:, col : col + 1],
+                        bias=be1_col[:, col : col + 1],
+                    )
+            planes_of[i] = planes
+
+        def group_h(i):
+            h_grouped = hq_pool.tile([P, F_PASSES, P, PACK], BF16, align_bytes=64)
+            nc.vector.tensor_copy(out=h_grouped[:], in_=planes_of[i][:].rearrange("p g t r -> p g r t"))
+            hg_of[i] = h_grouped
+
+        def quantise_h(i):
+            h_words = hq_pool.tile([P, F_PASSES * P], U32, align_bytes=64)
+            h_scales = hq_pool.tile([P, F_PASSES * P], U8, align_bytes=64)
+            nc.vector.quantize_mx(
+                out=h_words[:].bitcast(FP8X4),
+                scales=h_scales[:],
+                in_=hg_of[i][:].rearrange("p g r t -> p (g r t)"),
+            )
+            hq_of[i] = (h_words, h_scales)
+
+        def matmul_2(i):
+            h_words, h_scales = hq_of[i]
+            acc = psum_y.tile([P, D], F32)
+            for g in range(F_PASSES):
+                nc.tensor.matmul_mx(
+                    out=acc[:],
+                    lhsT=h_words[:, g * P : (g + 1) * P].bitcast(FP8X4),
+                    lhsT_scale=h_scales[:, g * P : (g + 1) * P],
+                    rhs=w2_words[:, g, :].bitcast(FP8X4),
+                    rhs_scale=w2_scales[:, g, :],
+                    start=(g == 0),
+                    stop=(g == F_PASSES - 1),
+                )
+            acc2_of[i] = acc
+
+        def add_b2(i):
+            y = outs.tile([P, D], F32)
+            sum_y = stats.tile([P, 1], F32)
+            nc.vector.scalar_tensor_tensor(
+                out=y[:], in0=acc2_of[i][:], scalar=1.0, in1=b2_bc[:], op0=ALU.mult, op1=ALU.add, accum_out=sum_y[:]
+            )
+            neg_mean2 = stats.tile([P, 1], F32)
+            nc.vector.tensor_scalar(
+                out=neg_mean2[:], in0=sum_y[:], scalar1=-1.0 / D, scalar2=None, op0=ALU.mult
+            )
+            y_of[i] = y
+            mean2_of[i] = neg_mean2
+
+        def moments_2(i):
+            sum_sq2 = stats.tile([P, 1], F32)
+            nc.scalar.activation(
+                out=junk[:, 0:D], in_=y_of[i][:], func=ACT.Square, bias=mean2_of[i][:], accum_out=sum_sq2[:]
+            )
+            sq2_of[i] = sum_sq2
+
+        def centre_times_g2(i):
+            scaled = outs.tile([P, D], F32)
+            nc.vector.scalar_tensor_tensor(
+                out=scaled[:], in0=y_of[i][:], scalar=mean2_of[i][:], in1=g2_bc[:], op0=ALU.add, op1=ALU.mult
+            )
+            scaled_of[i] = scaled
+
+        def inv_std_2(i):
+            rstd2_of[i] = inv_std(sq2_of[i], D)
+
+        def finish(i):
+            result = outs.tile([P, D], F32)
+            nc.vector.scalar_tensor_tensor(
+                out=result[:], in0=scaled_of[i][:], scalar=rstd2_of[i][:], in1=be2_bc[:], op0=ALU.mult, op1=ALU.add
+            )
+            nc.sync.dma_start(out=out_rows[:, i, :], in_=result[:])
+
+        def when_live(stage, i):
+            if 0 <= i < ROW_TILES:
+                stage(i)
+
+        ctx.enter_context(tc.manual_schedule())
+        for k in range(-2, ROW_TILES + 7):
+            when_live(inv_std_2, k - 6)
+            when_live(group_h, k - 4)
+            when_live(matmul_1, k)
+            when_live(transpose_n, k - 3)
+            when_live(gelu_and_moments, k - 1)
+            when_live(normalise_1, k - 2)
+            when_live(centre_times_g2, k - 5)
+            when_live(quantise_h, k - 4)
+            when_live(matmul_2, k - 4)
+            when_live(transpose_z, k + 2)
+            when_live(group_z, k + 1)
+            when_live(finish, k - 6)
+            when_live(quantise_z, k + 1)
+            when_live(add_b1, k)
+            when_live(scale_shift_1, k - 3)
+            when_live(add_b2, k - 4)
+            when_live(moments_2, k - 5)

@@ -184,7 +184,7 @@ def tile_emaaggregator_pa_t_kernel(
         def normalise_1(i):
             rstd = inv_std(sq1_of[i], F)
             n = wide.tile([P, F_PASSES, PACK, P], F32)
-            nc.gpsimd.tensor_scalar(
+            nc.vector.tensor_scalar(
                 out=flat(n),
                 in0=flat(x_of[i]),
                 scalar1=mean1_of[i][:],

@@ -36,7 +36,7 @@ def tile_emaaggregator_pa_t_kernel(
         wide = ctx.enter_context(tc.tile_pool(name="wide", bufs=4))
         hq_pool = ctx.enter_context(tc.tile_pool(name="hq", bufs=3))
         outs = ctx.enter_context(tc.tile_pool(name="outs", bufs=4))
-        stats = ctx.enter_context(tc.tile_pool(name="stats", bufs=6))
+        stats = ctx.enter_context(tc.tile_pool(name="stats", bufs=8))
         psum_z = ctx.enter_context(tc.psum_pool(name="psum_z", bufs=1))
         psum_s1 = ctx.enter_context(tc.psum_pool(name="psum_s1", bufs=3))
         psum_ht = ctx.enter_context(tc.psum_pool(name="psum_ht", bufs=2))
@@ -93,10 +93,6 @@ def tile_emaaggregator_pa_t_kernel(
         nc.scalar.dma_start(out=g2_bc[:], in_=g2.partition_broadcast(P))
         be2_bc = consts.tile([P, D], BF16)
         nc.scalar.dma_start(out=be2_bc[:], in_=be2.partition_broadcast(P))
-        b1_gtp = consts.tile([P, F_PASSES, PACK, P], BF16)
-        nc.vector.tensor_copy(
-            out=b1_gtp[:], in_=b1_bc[:].rearrange("r (g p t) -> r g t p", g=F_PASSES, t=PACK)
-        )
         g1_col = consts.tile([P, F_PASSES * PACK], F32)
         nc.vector.tensor_copy(out=g1_col[:], in_=g1_raw[:].rearrange("p g t -> p (g t)"))
         be1_col = consts.tile([P, F_PASSES * PACK], F32)
@@ -104,13 +100,10 @@ def tile_emaaggregator_pa_t_kernel(
 
         junk = consts.tile([P, F], BF16)
 
-        zt_of, zg_of, zq_of, acc1_of, x_of, mean1_of, sq1_of, n_of = {}, {}, {}, {}, {}, {}, {}, {}
+        zt_of, zg_of, zq_of, acc1_of, x_of, mean1_of, sq1_of, rstd1_of, n_of = {}, {}, {}, {}, {}, {}, {}, {}, {}
         ht_of, planes_of, hg_of, hq_of, acc2_of, y_of, mean2_of, sq2_of, rstd2_of, scaled_of = (
             {}, {}, {}, {}, {}, {}, {}, {}, {}, {},
         )
-
-        def flat(tile4):
-            return tile4[:].rearrange("r g t p -> r (g t p)")
 
         def transpose_z(i):
             zt = psum_z.tile([P, 2, P], F32)
@@ -121,7 +114,7 @@ def tile_emaaggregator_pa_t_kernel(
 
         def group_z(i):
             z_grouped = zq_pool.tile([P, P, 2], F32, align_bytes=64)
-            nc.vector.tensor_copy(out=z_grouped[:], in_=zt_of[i][:].rearrange("p u r -> p r u"))
+            nc.scalar.copy(out=z_grouped[:], in_=zt_of[i][:].rearrange("p u r -> p r u"))
             zg_of[i] = z_grouped
 
         def quantise_z(i):
@@ -151,18 +144,14 @@ def tile_emaaggregator_pa_t_kernel(
                 acc1_of[i].append(acc)
 
         def add_b1(i):
-            x = wide.tile([P, F_PASSES, PACK, P], F32)
+            x = wide.tile([P, F], F32)
             for g in range(F_PASSES):
-                nc.vector.tensor_tensor(
-                    out=x[:, g],
-                    in0=acc1_of[i][g][:].rearrange("r (p t) -> r t p", t=PACK),
-                    in1=b1_gtp[:, g],
-                    op=ALU.add,
-                )
+                cols = slice(g * K_PASS, (g + 1) * K_PASS)
+                nc.vector.tensor_tensor(out=x[:, cols], in0=acc1_of[i][g][:], in1=b1_bc[:, cols], op=ALU.add)
             x_of[i] = x
 
         def gelu_and_moments(i):
-            x_flat = flat(x_of[i])
+            x_flat = x_of[i][:]
             sum_x = stats.tile([P, 1], F32)
             nc.scalar.activation(out=x_flat, in_=x_flat, func=ACT.Gelu, accum_out=sum_x[:])
             neg_mean = stats.tile([P, 1], F32)
@@ -181,14 +170,16 @@ def tile_emaaggregator_pa_t_kernel(
             nc.gpsimd.tensor_tensor(out=rstd[:], in0=var[:], in1=neg_half[:], op=ALU.pow)
             return rstd
 
+        def inv_std_1(i):
+            rstd1_of[i] = inv_std(sq1_of[i], F)
+
         def normalise_1(i):
-            rstd = inv_std(sq1_of[i], F)
-            n = wide.tile([P, F_PASSES, PACK, P], F32)
+            n = wide.tile([P, F], F32)
             nc.vector.tensor_scalar(
-                out=flat(n),
-                in0=flat(x_of[i]),
+                out=n[:],
+                in0=x_of[i][:],
                 scalar1=mean1_of[i][:],
-                scalar2=rstd[:],
+                scalar2=rstd1_of[i][:],
                 op0=ALU.add,
                 op1=ALU.mult,
             )
@@ -199,7 +190,7 @@ def tile_emaaggregator_pa_t_kernel(
             for g in range(F_PASSES):
                 ht = psum_ht.tile([P, PACK, P], F32)
                 for t in range(PACK):
-                    nc.tensor.transpose(ht[:, t, :], n_of[i][:, g, t, :], ident[:])
+                    nc.tensor.transpose(ht[:, t, :], n_of[i][:, g * K_PASS + t : (g + 1) * K_PASS : PACK], ident[:])
                 ht_of[i].append(ht)
 
         def scale_shift_1(i):
@@ -288,21 +279,22 @@ def tile_emaaggregator_pa_t_kernel(
                 stage(i)
 
         ctx.enter_context(tc.manual_schedule())
-        for k in range(-2, ROW_TILES + 7):
-            when_live(inv_std_2, k - 6)
-            when_live(group_h, k - 4)
+        for k in range(-3, ROW_TILES + 8):
             when_live(matmul_1, k)
             when_live(transpose_n, k - 3)
+            when_live(moments_2, k - 6)
+            when_live(inv_std_2, k - 6)
+            when_live(group_z, k + 2)
+            when_live(transpose_z, k + 3)
             when_live(gelu_and_moments, k - 1)
+            when_live(inv_std_1, k - 1)
+            when_live(centre_times_g2, k - 6)
+            when_live(finish, k - 7)
             when_live(normalise_1, k - 2)
-            when_live(centre_times_g2, k - 5)
-            when_live(quantise_h, k - 4)
-            when_live(matmul_2, k - 4)
-            when_live(transpose_z, k + 2)
-            when_live(group_z, k + 1)
-            when_live(finish, k - 6)
+            when_live(add_b2, k - 5)
+            when_live(group_h, k - 4)
             when_live(quantise_z, k + 1)
             when_live(add_b1, k)
+            when_live(quantise_h, k - 4)
+            when_live(matmul_2, k - 4)
             when_live(scale_shift_1, k - 3)
-            when_live(add_b2, k - 4)
-            when_live(moments_2, k - 5)

@@ -38,9 +38,9 @@ def tile_emaaggregator_pa_t_kernel(
         outs = ctx.enter_context(tc.tile_pool(name="outs", bufs=4))
         stats = ctx.enter_context(tc.tile_pool(name="stats", bufs=8))
         psum_z = ctx.enter_context(tc.psum_pool(name="psum_z", bufs=1))
-        psum_s1 = ctx.enter_context(tc.psum_pool(name="psum_s1", bufs=3))
-        psum_ht = ctx.enter_context(tc.psum_pool(name="psum_ht", bufs=2))
-        psum_y = ctx.enter_context(tc.psum_pool(name="psum_y", bufs=2))
+        psum_s1 = ctx.enter_context(tc.psum_pool(name="psum_s1", bufs=2))
+        psum_ht = ctx.enter_context(tc.psum_pool(name="psum_ht", bufs=4))
+        psum_y = ctx.enter_context(tc.psum_pool(name="psum_y", bufs=1))
 
         z_rows = z.rearrange("(p i) k -> p i k", i=ROW_TILES)
         out_rows = out.rearrange("(p i) d -> p i d", i=ROW_TILES)
@@ -209,7 +209,10 @@ def tile_emaaggregator_pa_t_kernel(
 
         def group_h(i):
             h_grouped = hq_pool.tile([P, F_PASSES, P, PACK], BF16, align_bytes=64)
-            nc.vector.tensor_copy(out=h_grouped[:], in_=planes_of[i][:].rearrange("p g t r -> p g r t"))
+            nc.vector.tensor_copy(
+                out=h_grouped[:].rearrange("p g (c i) t -> p g c t i", i=4),
+                in_=planes_of[i][:].rearrange("p g t (c i) -> p g c t i", i=4),
+            )
             hg_of[i] = h_grouped
 
         def quantise_h(i):
@@ -279,22 +282,22 @@ def tile_emaaggregator_pa_t_kernel(
                 stage(i)
 
         ctx.enter_context(tc.manual_schedule())
-        for k in range(-3, ROW_TILES + 8):
-            when_live(matmul_1, k)
+        for k in range(-3, ROW_TILES + 9):
             when_live(transpose_n, k - 3)
-            when_live(moments_2, k - 6)
-            when_live(inv_std_2, k - 6)
             when_live(group_z, k + 2)
             when_live(transpose_z, k + 3)
+            when_live(scale_shift_1, k - 4)
+            when_live(moments_2, k - 7)
+            when_live(inv_std_2, k - 7)
+            when_live(matmul_1, k)
             when_live(gelu_and_moments, k - 1)
             when_live(inv_std_1, k - 1)
-            when_live(centre_times_g2, k - 6)
-            when_live(finish, k - 7)
+            when_live(add_b2, k - 6)
+            when_live(centre_times_g2, k - 7)
+            when_live(finish, k - 8)
+            when_live(group_h, k - 5)
             when_live(normalise_1, k - 2)
-            when_live(add_b2, k - 5)
-            when_live(group_h, k - 4)
+            when_live(quantise_h, k - 5)
+            when_live(matmul_2, k - 5)
             when_live(quantise_z, k + 1)
             when_live(add_b1, k)
-            when_live(quantise_h, k - 4)
-            when_live(matmul_2, k - 4)
-            when_live(scale_shift_1, k - 3)

@@ -33,14 +33,15 @@ def tile_emaaggregator_pa_t_kernel(
     with ExitStack() as ctx:
         consts = ctx.enter_context(tc.tile_pool(name="consts", bufs=1))
         zq_pool = ctx.enter_context(tc.tile_pool(name="zq", bufs=3))
-        wide = ctx.enter_context(tc.tile_pool(name="wide", bufs=4))
+        wide = ctx.enter_context(tc.tile_pool(name="wide", bufs=5))
+        plane_pool = ctx.enter_context(tc.tile_pool(name="planes", bufs=3))
         hq_pool = ctx.enter_context(tc.tile_pool(name="hq", bufs=3))
         outs = ctx.enter_context(tc.tile_pool(name="outs", bufs=4))
         stats = ctx.enter_context(tc.tile_pool(name="stats", bufs=8))
         psum_z = ctx.enter_context(tc.psum_pool(name="psum_z", bufs=1))
-        psum_s1 = ctx.enter_context(tc.psum_pool(name="psum_s1", bufs=2))
-        psum_ht = ctx.enter_context(tc.psum_pool(name="psum_ht", bufs=4))
-        psum_y = ctx.enter_context(tc.psum_pool(name="psum_y", bufs=1))
+        psum_s1 = ctx.enter_context(tc.psum_pool(name="psum_s1", bufs=3))
+        psum_ht = ctx.enter_context(tc.psum_pool(name="psum_ht", bufs=2))
+        psum_y = ctx.enter_context(tc.psum_pool(name="psum_y", bufs=2))
 
         z_rows = z.rearrange("(p i) k -> p i k", i=ROW_TILES)
         out_rows = out.rearrange("(p i) d -> p i d", i=ROW_TILES)
@@ -100,6 +101,7 @@ def tile_emaaggregator_pa_t_kernel(
 
         junk = consts.tile([P, F], BF16)
 
+        sum1_of, sum2_of = {}, {}
         zt_of, zg_of, zq_of, acc1_of, x_of, mean1_of, sq1_of, rstd1_of, n_of = {}, {}, {}, {}, {}, {}, {}, {}, {}
         ht_of, planes_of, hg_of, hq_of, acc2_of, y_of, mean2_of, sq2_of, rstd2_of, scaled_of = (
             {}, {}, {}, {}, {}, {}, {}, {}, {}, {},
@@ -150,15 +152,26 @@ def tile_emaaggregator_pa_t_kernel(
                 nc.vector.tensor_tensor(out=x[:, cols], in0=acc1_of[i][g][:], in1=b1_bc[:, cols], op=ALU.add)
             x_of[i] = x
 
-        def gelu_and_moments(i):
-            x_flat = x_of[i][:]
+        def gelu(i):
             sum_x = stats.tile([P, 1], F32)
-            nc.scalar.activation(out=x_flat, in_=x_flat, func=ACT.Gelu, accum_out=sum_x[:])
+            nc.scalar.activation(out=x_of[i][:], in_=x_of[i][:], func=ACT.Gelu, accum_out=sum_x[:])
+            sum1_of[i] = sum_x
+
+        def minus_mean(total, width):
             neg_mean = stats.tile([P, 1], F32)
-            nc.scalar.mul(out=neg_mean[:], in_=sum_x[:], mul=-1.0 / F)
+            nc.gpsimd.tensor_scalar(
+                out=neg_mean[:], in0=total[:], scalar1=-1.0 / width, scalar2=0.0, op0=ALU.mult, op1=ALU.add
+            )
+            return neg_mean
+
+        def mean_1(i):
+            mean1_of[i] = minus_mean(sum1_of[i], F)
+
+        def moments_1(i):
             sum_sq = stats.tile([P, 1], F32)
-            nc.scalar.activation(out=junk[:], in_=x_flat, func=ACT.Square, bias=neg_mean[:], accum_out=sum_sq[:])
-            mean1_of[i] = neg_mean
+            nc.scalar.activation(
+                out=junk[:], in_=x_of[i][:], func=ACT.Square, bias=mean1_of[i][:], accum_out=sum_sq[:]
+            )
             sq1_of[i] = sum_sq
 
         def inv_std(sum_sq, width):
@@ -185,33 +198,43 @@ def tile_emaaggregator_pa_t_kernel(
             )
             n_of[i] = n
 
-        def transpose_n(i):
-            ht_of[i] = []
-            for g in range(F_PASSES):
-                ht = psum_ht.tile([P, PACK, P], F32)
-                for t in range(PACK):
-                    nc.tensor.transpose(ht[:, t, :], n_of[i][:, g * K_PASS + t : (g + 1) * K_PASS : PACK], ident[:])
-                ht_of[i].append(ht)
+        def transpose_n(u):
+            pair, g = divmod(u, 2)
+            ht_of[u] = []
+            for half in range(2):
+                ht = psum_ht.tile([P, 2, 2, P], F32)
+                for tl in range(2):
+                    t = 2 * half + tl
+                    for j in range(2):
+                        nc.tensor.transpose(
+                            ht[:, tl, j, :],
+                            n_of[2 * pair + j][:, g * K_PASS + t : (g + 1) * K_PASS : PACK],
+                            ident[:],
+                        )
+                ht_of[u].append(ht)
 
-        def scale_shift_1(i):
-            planes = hq_pool.tile([P, F_PASSES, PACK, P], BF16)
-            for g in range(F_PASSES):
-                for t in range(PACK):
+        def scale_shift_1(u):
+            pair, g = divmod(u, 2)
+            if g == 0:
+                planes = plane_pool.tile([P, F_PASSES, PACK, 2, P], BF16)
+                planes_of[pair] = planes
+            for half in range(2):
+                for tl in range(2):
+                    t = 2 * half + tl
                     col = g * PACK + t
                     nc.scalar.activation(
-                        out=planes[:, g, t, :],
-                        in_=ht_of[i][g][:, t, :],
+                        out=planes_of[pair][:, g, t, :, :],
+                        in_=ht_of[u][half][:, tl, :, :],
                         func=ACT.Identity,
                         scale=g1_col[:, col : col + 1],
                         bias=be1_col[:, col : col + 1],
                     )
-            planes_of[i] = planes
 
         def group_h(i):
             h_grouped = hq_pool.tile([P, F_PASSES, P, PACK], BF16, align_bytes=64)
             nc.vector.tensor_copy(
                 out=h_grouped[:].rearrange("p g (c i) t -> p g c t i", i=4),
-                in_=planes_of[i][:].rearrange("p g t (c i) -> p g c t i", i=4),
+                in_=planes_of[i // 2][:, :, :, i % 2, :].rearrange("p g t (c i) -> p g c t i", i=4),
             )
             hg_of[i] = h_grouped
 
@@ -246,12 +269,11 @@ def tile_emaaggregator_pa_t_kernel(
             nc.vector.scalar_tensor_tensor(
                 out=y[:], in0=acc2_of[i][:], scalar=1.0, in1=b2_bc[:], op0=ALU.mult, op1=ALU.add, accum_out=sum_y[:]
             )
-            neg_mean2 = stats.tile([P, 1], F32)
-            nc.vector.tensor_scalar(
-                out=neg_mean2[:], in0=sum_y[:], scalar1=-1.0 / D, scalar2=None, op0=ALU.mult
-            )
             y_of[i] = y
-            mean2_of[i] = neg_mean2
+            sum2_of[i] = sum_y
+
+        def mean_2(i):
+            mean2_of[i] = minus_mean(sum2_of[i], D)
 
         def moments_2(i):
             sum_sq2 = stats.tile([P, 1], F32)
@@ -282,22 +304,25 @@ def tile_emaaggregator_pa_t_kernel(
                 stage(i)
 
         ctx.enter_context(tc.manual_schedule())
-        for k in range(-3, ROW_TILES + 9):
-            when_live(transpose_n, k - 3)
+        for k in range(-3, ROW_TILES + 10):
+            when_live(matmul_1, k)
+            when_live(transpose_n, k - 4)
+            when_live(gelu, k - 1)
+            when_live(mean_1, k - 1)
+            when_live(moments_2, k - 8)
+            when_live(inv_std_2, k - 8)
             when_live(group_z, k + 2)
             when_live(transpose_z, k + 3)
-            when_live(scale_shift_1, k - 4)
-            when_live(moments_2, k - 7)
-            when_live(inv_std_2, k - 7)
-            when_live(matmul_1, k)
-            when_live(gelu_and_moments, k - 1)
-            when_live(inv_std_1, k - 1)
-            when_live(add_b2, k - 6)
-            when_live(centre_times_g2, k - 7)
-            when_live(finish, k - 8)
-            when_live(group_h, k - 5)
+            when_live(moments_1, k - 1)
+            when_live(centre_times_g2, k - 8)
+            when_live(finish, k - 9)
             when_live(normalise_1, k - 2)
-            when_live(quantise_h, k - 5)
-            when_live(matmul_2, k - 5)
+            when_live(add_b2, k - 7)
+            when_live(mean_2, k - 7)
+            when_live(inv_std_1, k - 1)
+            when_live(group_h, k - 6)
             when_live(quantise_z, k + 1)
             when_live(add_b1, k)
+            when_live(quantise_h, k - 6)
+            when_live(matmul_2, k - 6)
+            when_live(scale_shift_1, k - 4)

@@ -50,7 +50,7 @@ def tile_emaaggregator_pa_t_kernel(
         w2_scales = consts.tile([P, F_PASSES, D], U8, align_bytes=64)
         nc.vector.memset(w1_scales[:].bitcast(I32), 0)
         nc.vector.memset(w2_scales[:].bitcast(I32), 0)
-        neg_half = consts.tile([P, 1], F32)
+        neg_half = consts.tile([P, 2], F32)
         nc.vector.memset(neg_half[:], -0.5)
         ident = consts.tile([P, P], F32)
         make_identity(nc, ident[:])
@@ -101,7 +101,7 @@ def tile_emaaggregator_pa_t_kernel(
 
         junk = consts.tile([P, F], BF16)
 
-        sum1_of, sum2_of = {}, {}
+        sum1_of, sum2_of, ve_of = {}, {}, {}
         zt_of, zg_of, zq_of, acc1_of, x_of, mean1_of, sq1_of, rstd1_of, n_of = {}, {}, {}, {}, {}, {}, {}, {}, {}
         ht_of, planes_of, hg_of, hq_of, acc2_of, y_of, mean2_of, sq2_of, rstd2_of, scaled_of = (
             {}, {}, {}, {}, {}, {}, {}, {}, {}, {},
@@ -159,9 +159,7 @@ def tile_emaaggregator_pa_t_kernel(
 
         def minus_mean(total, width):
             neg_mean = stats.tile([P, 1], F32)
-            nc.gpsimd.tensor_scalar(
-                out=neg_mean[:], in0=total[:], scalar1=-1.0 / width, scalar2=0.0, op0=ALU.mult, op1=ALU.add
-            )
+            nc.scalar.activation(out=neg_mean[:], in_=total[:], func=ACT.Copy, scale=-1.0 / width)
             return neg_mean
 
         def mean_1(i):
@@ -174,17 +172,31 @@ def tile_emaaggregator_pa_t_kernel(
             )
             sq1_of[i] = sum_sq
 
-        def inv_std(sum_sq, width):
-            var = stats.tile([P, 1], F32)
-            nc.gpsimd.tensor_scalar(
-                out=var[:], in0=sum_sq[:], scalar1=1.0 / width, scalar2=EPS, op0=ALU.mult, op1=ALU.add
-            )
-            rstd = stats.tile([P, 1], F32)
-            nc.gpsimd.tensor_tensor(out=rstd[:], in0=var[:], in1=neg_half[:], op=ALU.pow)
-            return rstd
+        def var_eps(k):
+            if k not in ve_of:
+                ve = stats.tile([P, 2], F32)
+                ve_of[k] = ve
+            return ve_of[k]
 
-        def inv_std_1(i):
-            rstd1_of[i] = inv_std(sq1_of[i], F)
+        def var_1(i, k):
+            nc.scalar.activation(
+                out=var_eps(k)[:, 0:1], in_=sq1_of[i][:], func=ACT.Copy, scale=1.0 / F, bias=EPS
+            )
+
+        def var_2(i, k):
+            nc.scalar.activation(
+                out=var_eps(k)[:, 1:2], in_=sq2_of[i][:], func=ACT.Copy, scale=1.0 / D, bias=EPS
+            )
+
+        def inv_std(k, i1, i2):
+            live1, live2 = 0 <= i1 < ROW_TILES, 0 <= i2 < ROW_TILES
+            if not (live1 or live2):
+                return
+            cols = slice(0 if live1 else 1, 2 if live2 else 1)
+            rstd = stats.tile([P, 2], F32)
+            nc.gpsimd.tensor_tensor(out=rstd[:, cols], in0=ve_of[k][:, cols], in1=neg_half[:, cols], op=ALU.pow)
+            rstd1_of[i1] = rstd[:, 0:1]
+            rstd2_of[i2] = rstd[:, 1:2]
 
         def normalise_1(i):
             n = wide.tile([P, F], F32)
@@ -192,7 +204,7 @@ def tile_emaaggregator_pa_t_kernel(
                 out=n[:],
                 in0=x_of[i][:],
                 scalar1=mean1_of[i][:],
-                scalar2=rstd1_of[i][:],
+                scalar2=rstd1_of[i],
                 op0=ALU.add,
                 op1=ALU.mult,
             )
@@ -213,12 +225,12 @@ def tile_emaaggregator_pa_t_kernel(
                         )
                 ht_of[u].append(ht)
 
-        def scale_shift_1(u):
+        def scale_shift_1(u, half):
             pair, g = divmod(u, 2)
-            if g == 0:
+            if g == 0 and half == 0:
                 planes = plane_pool.tile([P, F_PASSES, PACK, 2, P], BF16)
                 planes_of[pair] = planes
-            for half in range(2):
+            if True:
                 for tl in range(2):
                     t = 2 * half + tl
                     col = g * PACK + t
@@ -289,40 +301,39 @@ def tile_emaaggregator_pa_t_kernel(
             )
             scaled_of[i] = scaled
 
-        def inv_std_2(i):
-            rstd2_of[i] = inv_std(sq2_of[i], D)
-
         def finish(i):
             result = outs.tile([P, D], F32)
             nc.vector.scalar_tensor_tensor(
-                out=result[:], in0=scaled_of[i][:], scalar=rstd2_of[i][:], in1=be2_bc[:], op0=ALU.mult, op1=ALU.add
+                out=result[:], in0=scaled_of[i][:], scalar=rstd2_of[i], in1=be2_bc[:], op0=ALU.mult, op1=ALU.add
             )
             nc.sync.dma_start(out=out_rows[:, i, :], in_=result[:])
 
-        def when_live(stage, i):
+        def when_live(stage, i, *more):
             if 0 <= i < ROW_TILES:
-                stage(i)
+                stage(i, *more)
 
         ctx.enter_context(tc.manual_schedule())
-        for k in range(-3, ROW_TILES + 10):
+        for k in range(-3, ROW_TILES + 11):
             when_live(matmul_1, k)
             when_live(transpose_n, k - 4)
             when_live(gelu, k - 1)
-            when_live(mean_1, k - 1)
-            when_live(moments_2, k - 8)
-            when_live(inv_std_2, k - 8)
+            when_live(mean_2, k - 8)
             when_live(group_z, k + 2)
             when_live(transpose_z, k + 3)
+            when_live(mean_1, k - 1)
+            when_live(moments_2, k - 8)
             when_live(moments_1, k - 1)
-            when_live(centre_times_g2, k - 8)
-            when_live(finish, k - 9)
+            when_live(var_2, k - 8, k)
+            when_live(scale_shift_1, k - 4, 0)
+            when_live(var_1, k - 1, k)
+            inv_std(k, k - 1, k - 8)
+            when_live(scale_shift_1, k - 4, 1)
+            when_live(centre_times_g2, k - 9)
+            when_live(finish, k - 10)
             when_live(normalise_1, k - 2)
             when_live(add_b2, k - 7)
-            when_live(mean_2, k - 7)
-            when_live(inv_std_1, k - 1)
             when_live(group_h, k - 6)
             when_live(quantise_z, k + 1)
             when_live(add_b1, k)
             when_live(quantise_h, k - 6)
             when_live(matmul_2, k - 6)
-            when_live(scale_shift_1, k - 4)

@@ -32,12 +32,13 @@ def tile_emaaggregator_pa_t_kernel(
     nc = tc.nc
     with ExitStack() as ctx:
         consts = ctx.enter_context(tc.tile_pool(name="consts", bufs=1))
-        zq_pool = ctx.enter_context(tc.tile_pool(name="zq", bufs=3))
-        wide = ctx.enter_context(tc.tile_pool(name="wide", bufs=5))
+        zq_pool = ctx.enter_context(tc.tile_pool(name="zq", bufs=4))
+        wide = ctx.enter_context(tc.tile_pool(name="wide", bufs=6))
         plane_pool = ctx.enter_context(tc.tile_pool(name="planes", bufs=3))
         hq_pool = ctx.enter_context(tc.tile_pool(name="hq", bufs=3))
+        hg_pool = ctx.enter_context(tc.tile_pool(name="hg", bufs=1))
         outs = ctx.enter_context(tc.tile_pool(name="outs", bufs=4))
-        stats = ctx.enter_context(tc.tile_pool(name="stats", bufs=8))
+        stats = ctx.enter_context(tc.tile_pool(name="stats", bufs=12))
         psum_z = ctx.enter_context(tc.psum_pool(name="psum_z", bufs=1))
         psum_s1 = ctx.enter_context(tc.psum_pool(name="psum_s1", bufs=3))
         psum_ht = ctx.enter_context(tc.psum_pool(name="psum_ht", bufs=2))
@@ -116,7 +117,7 @@ def tile_emaaggregator_pa_t_kernel(
 
         def group_z(i):
             z_grouped = zq_pool.tile([P, P, 2], F32, align_bytes=64)
-            nc.scalar.copy(out=z_grouped[:], in_=zt_of[i][:].rearrange("p u r -> p r u"))
+            nc.vector.tensor_copy(out=z_grouped[:], in_=zt_of[i][:].rearrange("p u r -> p r u"))
             zg_of[i] = z_grouped
 
         def quantise_z(i):
@@ -194,7 +195,7 @@ def tile_emaaggregator_pa_t_kernel(
                 return
             cols = slice(0 if live1 else 1, 2 if live2 else 1)
             rstd = stats.tile([P, 2], F32)
-            nc.gpsimd.tensor_tensor(out=rstd[:, cols], in0=ve_of[k][:, cols], in1=neg_half[:, cols], op=ALU.pow)
+            nc.gpsimd.tensor_tensor(out=rstd[:, cols], in0=ve_of[k - 1][:, cols], in1=neg_half[:, cols], op=ALU.pow)
             rstd1_of[i1] = rstd[:, 0:1]
             rstd2_of[i2] = rstd[:, 1:2]
 
@@ -243,10 +244,14 @@ def tile_emaaggregator_pa_t_kernel(
                     )
 
         def group_h(i):
-            h_grouped = hq_pool.tile([P, F_PASSES, P, PACK], BF16, align_bytes=64)
-            nc.vector.tensor_copy(
-                out=h_grouped[:].rearrange("p g (c i) t -> p g c t i", i=4),
-                in_=planes_of[i // 2][:, :, :, i % 2, :].rearrange("p g t (c i) -> p g c t i", i=4),
+            h_grouped = hg_pool.tile([P, F_PASSES, P, PACK], BF16, align_bytes=64)
+            nc.gpsimd.tensor_scalar(
+                out=h_grouped[:],
+                in0=planes_of[i // 2][:, :, :, i % 2, :].rearrange("p g t r -> p g r t"),
+                scalar1=1.0,
+                scalar2=0.0,
+                op0=ALU.mult,
+                op1=ALU.add,
             )
             hg_of[i] = h_grouped
 
@@ -313,27 +318,27 @@ def tile_emaaggregator_pa_t_kernel(
                 stage(i, *more)
 
         ctx.enter_context(tc.manual_schedule())
-        for k in range(-3, ROW_TILES + 11):
-            when_live(matmul_1, k)
-            when_live(transpose_n, k - 4)
-            when_live(gelu, k - 1)
-            when_live(mean_2, k - 8)
-            when_live(group_z, k + 2)
-            when_live(transpose_z, k + 3)
-            when_live(mean_1, k - 1)
-            when_live(moments_2, k - 8)
-            when_live(moments_1, k - 1)
-            when_live(var_2, k - 8, k)
-            when_live(scale_shift_1, k - 4, 0)
-            when_live(var_1, k - 1, k)
-            inv_std(k, k - 1, k - 8)
-            when_live(scale_shift_1, k - 4, 1)
-            when_live(centre_times_g2, k - 9)
-            when_live(finish, k - 10)
-            when_live(normalise_1, k - 2)
-            when_live(add_b2, k - 7)
-            when_live(group_h, k - 6)
-            when_live(quantise_z, k + 1)
+        for k in range(-4, ROW_TILES + 15):
             when_live(add_b1, k)
-            when_live(quantise_h, k - 6)
-            when_live(matmul_2, k - 6)
+            when_live(matmul_1, k + 1)
+            when_live(add_b2, k - 11)
+            when_live(matmul_2, k - 10)
+            when_live(group_z, k + 3)
+            when_live(transpose_z, k + 4)
+            when_live(group_h, k - 9)
+            inv_std(k, k - 3, k - 13)
+            when_live(scale_shift_1, k - 7, 0)
+            when_live(scale_shift_1, k - 7, 1)
+            when_live(transpose_n, k - 6)
+            when_live(gelu, k - 1)
+            when_live(moments_1, k - 2)
+            when_live(mean_1, k - 1)
+            when_live(moments_2, k - 12)
+            when_live(var_1, k - 2, k)
+            when_live(mean_2, k - 11)
+            when_live(var_2, k - 12, k)
+            when_live(normalise_1, k - 4)
+            when_live(centre_times_g2, k - 12)
+            when_live(finish, k - 14)
+            when_live(quantise_z, k + 2)
+            when_live(quantise_h, k - 9)

@@ -117,7 +117,7 @@ def tile_emaaggregator_pa_t_kernel(
 
         def group_z(i):
             z_grouped = zq_pool.tile([P, P, 2], F32, align_bytes=64)
-            nc.vector.tensor_copy(out=z_grouped[:], in_=zt_of[i][:].rearrange("p u r -> p r u"))
+            nc.scalar.copy(out=z_grouped[:], in_=zt_of[i][:].rearrange("p u r -> p r u"))
             zg_of[i] = z_grouped
 
         def quantise_z(i):
@@ -228,19 +228,28 @@ def tile_emaaggregator_pa_t_kernel(
 
         def scale_shift_1(u, half):
             pair, g = divmod(u, 2)
-            if g == 0 and half == 0:
+            if pair not in planes_of:
                 planes = plane_pool.tile([P, F_PASSES, PACK, 2, P], BF16)
                 planes_of[pair] = planes
-            if True:
-                for tl in range(2):
-                    t = 2 * half + tl
-                    col = g * PACK + t
+            for tl in range(2):
+                t = 2 * half + tl
+                col = g * PACK + t
+                if half == 0:
                     nc.scalar.activation(
                         out=planes_of[pair][:, g, t, :, :],
                         in_=ht_of[u][half][:, tl, :, :],
                         func=ACT.Identity,
                         scale=g1_col[:, col : col + 1],
                         bias=be1_col[:, col : col + 1],
+                    )
+                else:
+                    nc.vector.tensor_scalar(
+                        out=planes_of[pair][:, g, t, :, :],
+                        in0=ht_of[u][half][:, tl, :, :],
+                        scalar1=g1_col[:, col : col + 1],
+                        scalar2=be1_col[:, col : col + 1],
+                        op0=ALU.mult,
+                        op1=ALU.add,
                     )
 
         def group_h(i):
@@ -323,13 +332,13 @@ def tile_emaaggregator_pa_t_kernel(
             when_live(matmul_1, k + 1)
             when_live(add_b2, k - 11)
             when_live(matmul_2, k - 10)
-            when_live(group_z, k + 3)
-            when_live(transpose_z, k + 4)
+            when_live(scale_shift_1, k - 7, 1)
             when_live(group_h, k - 9)
             inv_std(k, k - 3, k - 13)
             when_live(scale_shift_1, k - 7, 0)
-            when_live(scale_shift_1, k - 7, 1)
             when_live(transpose_n, k - 6)
+            when_live(group_z, k + 3)
+            when_live(transpose_z, k + 4)
             when_live(gelu, k - 1)
             when_live(moments_1, k - 2)
             when_live(mean_1, k - 1)

@@ -47,9 +47,10 @@ def tile_emaaggregator_pa_t_kernel(
         z_rows = z.rearrange("(p i) k -> p i k", i=ROW_TILES)
         out_rows = out.rearrange("(p i) d -> p i d", i=ROW_TILES)
 
+        w1_scales_raw = consts.tile([P, F], U8, align_bytes=64)
         w1_scales = consts.tile([P, F], U8, align_bytes=64)
         w2_scales = consts.tile([P, F_PASSES, D], U8, align_bytes=64)
-        nc.vector.memset(w1_scales[:].bitcast(I32), 0)
+        nc.vector.memset(w1_scales_raw[:].bitcast(I32), 0)
         nc.vector.memset(w2_scales[:].bitcast(I32), 0)
         neg_half = consts.tile([P, 2], F32)
         nc.vector.memset(neg_half[:], -0.5)
@@ -57,17 +58,27 @@ def tile_emaaggregator_pa_t_kernel(
         make_identity(nc, ident[:])
 
         z_sb = consts.tile([P, ROW_TILES, D], BF16)
-        nc.sync.dma_start(out=z_sb[:, 0:Z_CHUNK, :], in_=z_rows[:, 0:Z_CHUNK, :])
-        w1_words = consts.tile([P, F], U32, align_bytes=64)
+        nc.sync.dma_start(out=z_sb[:, 0:1, :], in_=z_rows[:, 0:1, :])
+        w1_words_raw = consts.tile([P, F], U32, align_bytes=64)
         nc.sync.dma_start(
-            out=w1_words[:].bitcast(I32),
+            out=w1_words_raw[:].bitcast(I32),
             in_=W1_words[0].rearrange("p n t -> p (n t)").bitcast(I32),
         )
         for q in range(4):
             nc.sync.dma_start(
-                out=w1_scales[32 * q : 32 * q + 4, :].bitcast(I32),
+                out=w1_scales_raw[32 * q : 32 * q + 4, :].bitcast(I32),
                 in_=W1_scales[0, 4 * q : 4 * q + 4, :].bitcast(I32),
             )
+        w1_words = consts.tile([P, F], U32, align_bytes=64)
+        nc.vector.tensor_copy(
+            out=w1_words[:].bitcast(I32).rearrange("p (g t m) -> p g t m", g=F_PASSES, t=PACK),
+            in_=w1_words_raw[:].bitcast(I32).rearrange("p (g m t) -> p g t m", g=F_PASSES, t=PACK),
+        )
+        nc.vector.tensor_copy(
+            out=w1_scales[:].rearrange("p (g t m) -> p g t m", g=F_PASSES, t=PACK),
+            in_=w1_scales_raw[:].rearrange("p (g m t) -> p g t m", g=F_PASSES, t=PACK),
+        )
+        nc.sync.dma_start(out=z_sb[:, 1:Z_CHUNK, :], in_=z_rows[:, 1:Z_CHUNK, :])
         w2_words = consts.tile([P, F_PASSES, D], U32, align_bytes=64)
         for g in range(F_PASSES):
             nc.sync.dma_start(
@@ -83,18 +94,23 @@ def tile_emaaggregator_pa_t_kernel(
             rows = slice(c * Z_CHUNK, (c + 1) * Z_CHUNK)
             nc.sync.dma_start(out=z_sb[:, rows, :], in_=z_rows[:, rows, :])
 
-        b1_bc = consts.tile([P, F], BF16)
-        nc.scalar.dma_start(out=b1_bc[:], in_=b1.partition_broadcast(P))
+        b1_raw = consts.tile([P, F], BF16)
+        nc.scalar.dma_start(out=b1_raw[:], in_=b1.partition_broadcast(P))
         g1_raw = consts.tile([P, F_PASSES, PACK], BF16)
         nc.scalar.dma_start(out=g1_raw[:], in_=g1.rearrange("(g p t) -> p g t", g=F_PASSES, t=PACK))
         be1_raw = consts.tile([P, F_PASSES, PACK], BF16)
         nc.scalar.dma_start(out=be1_raw[:], in_=be1.rearrange("(g p t) -> p g t", g=F_PASSES, t=PACK))
         b2_bc = consts.tile([P, D], BF16)
-        nc.scalar.dma_start(out=b2_bc[:], in_=b2.partition_broadcast(P))
         g2_bc = consts.tile([P, D], BF16)
-        nc.scalar.dma_start(out=g2_bc[:], in_=g2.partition_broadcast(P))
         be2_bc = consts.tile([P, D], BF16)
-        nc.scalar.dma_start(out=be2_bc[:], in_=be2.partition_broadcast(P))
+        warm = consts.tile([P, 1], F32)
+        nc.vector.memset(warm[:], 0.0)
+        nc.scalar.activation(out=warm[:], in_=warm[:], func=ACT.Gelu)
+        b1_bc = consts.tile([P, F], BF16)
+        nc.scalar.copy(
+            out=b1_bc[:].rearrange("p (g t m) -> p g t m", g=F_PASSES, t=PACK),
+            in_=b1_raw[:].rearrange("p (g m t) -> p g t m", g=F_PASSES, t=PACK),
+        )
         g1_col = consts.tile([P, F_PASSES * PACK], F32)
         nc.vector.tensor_copy(out=g1_col[:], in_=g1_raw[:].rearrange("p g t -> p (g t)"))
         be1_col = consts.tile([P, F_PASSES * PACK], F32)
@@ -115,9 +131,12 @@ def tile_emaaggregator_pa_t_kernel(
                 nc.tensor.transpose(zt[:, u, :], words[:, u : D // 2 : 2], ident[:])
             zt_of[i] = zt
 
-        def group_z(i):
+        def group_z(i, on_vector):
             z_grouped = zq_pool.tile([P, P, 2], F32, align_bytes=64)
-            nc.scalar.copy(out=z_grouped[:], in_=zt_of[i][:].rearrange("p u r -> p r u"))
+            if on_vector:
+                nc.vector.tensor_copy(out=z_grouped[:], in_=zt_of[i][:].rearrange("p u r -> p r u"))
+            else:
+                nc.scalar.copy(out=z_grouped[:], in_=zt_of[i][:].rearrange("p u r -> p r u"))
             zg_of[i] = z_grouped
 
         def quantise_z(i):
@@ -221,12 +240,12 @@ def tile_emaaggregator_pa_t_kernel(
                     for j in range(2):
                         nc.tensor.transpose(
                             ht[:, tl, j, :],
-                            n_of[2 * pair + j][:, g * K_PASS + t : (g + 1) * K_PASS : PACK],
+                            n_of[2 * pair + j][:, g * K_PASS + t * P : g * K_PASS + (t + 1) * P],
                             ident[:],
                         )
                 ht_of[u].append(ht)
 
-        def scale_shift_1(u, half):
+        def scale_shift_1(u, half, on_vector):
             pair, g = divmod(u, 2)
             if pair not in planes_of:
                 planes = plane_pool.tile([P, F_PASSES, PACK, 2, P], BF16)
@@ -234,7 +253,7 @@ def tile_emaaggregator_pa_t_kernel(
             for tl in range(2):
                 t = 2 * half + tl
                 col = g * PACK + t
-                if half == 0:
+                if not on_vector:
                     nc.scalar.activation(
                         out=planes_of[pair][:, g, t, :, :],
                         in_=ht_of[u][half][:, tl, :, :],
@@ -328,17 +347,29 @@ def tile_emaaggregator_pa_t_kernel(
 
         ctx.enter_context(tc.manual_schedule())
         for k in range(-4, ROW_TILES + 15):
+            if k == 0:
+                nc.scalar.dma_start(out=b2_bc[:], in_=b2.partition_broadcast(P))
+                nc.scalar.dma_start(out=g2_bc[:], in_=g2.partition_broadcast(P))
+                nc.scalar.dma_start(out=be2_bc[:], in_=be2.partition_broadcast(P))
             when_live(add_b1, k)
             when_live(matmul_1, k + 1)
             when_live(add_b2, k - 11)
             when_live(matmul_2, k - 10)
-            when_live(scale_shift_1, k - 7, 1)
+            odd = k % 2 == 1
+            if odd:
+                when_live(scale_shift_1, k - 7, 1, True)
+            else:
+                when_live(group_z, k + 3, True)
+                when_live(transpose_z, k + 4)
             when_live(group_h, k - 9)
             inv_std(k, k - 3, k - 13)
-            when_live(scale_shift_1, k - 7, 0)
+            when_live(scale_shift_1, k - 7, 0, False)
+            if not odd:
+                when_live(scale_shift_1, k - 7, 1, False)
             when_live(transpose_n, k - 6)
-            when_live(group_z, k + 3)
-            when_live(transpose_z, k + 4)
+            if odd:
+                when_live(group_z, k + 3, False)
+                when_live(transpose_z, k + 4)
             when_live(gelu, k - 1)
             when_live(moments_1, k - 2)
             when_live(mean_1, k - 1)

@@ -40,13 +40,16 @@ def tile_emaaggregator_pa_t_kernel(
         outs = ctx.enter_context(tc.tile_pool(name="outs", bufs=4))
         stats = ctx.enter_context(tc.tile_pool(name="stats", bufs=12))
         psum_z = ctx.enter_context(tc.psum_pool(name="psum_z", bufs=1))
-        psum_s1 = ctx.enter_context(tc.psum_pool(name="psum_s1", bufs=3))
+        psum_s1 = ctx.enter_context(tc.psum_pool(name="psum_s1", bufs=2))
+        psum_c = ctx.enter_context(tc.psum_pool(name="psum_c", bufs=1))
         psum_ht = ctx.enter_context(tc.psum_pool(name="psum_ht", bufs=2))
         psum_y = ctx.enter_context(tc.psum_pool(name="psum_y", bufs=2))
 
         z_rows = z.rearrange("(p i) k -> p i k", i=ROW_TILES)
         out_rows = out.rearrange("(p i) d -> p i d", i=ROW_TILES)
 
+        warm = consts.tile([P, 1], F32)
+        nc.vector.memset(warm[:], 0.0)
         w1_scales_raw = consts.tile([P, F], U8, align_bytes=64)
         w1_scales = consts.tile([P, F], U8, align_bytes=64)
         w2_scales = consts.tile([P, F_PASSES, D], U8, align_bytes=64)
@@ -101,10 +104,13 @@ def tile_emaaggregator_pa_t_kernel(
         be1_raw = consts.tile([P, F_PASSES, PACK], BF16)
         nc.scalar.dma_start(out=be1_raw[:], in_=be1.rearrange("(g p t) -> p g t", g=F_PASSES, t=PACK))
         b2_bc = consts.tile([P, D], BF16)
-        g2_bc = consts.tile([P, D], BF16)
-        be2_bc = consts.tile([P, D], BF16)
-        warm = consts.tile([P, 1], F32)
-        nc.vector.memset(warm[:], 0.0)
+        ones = consts.tile([P, P], BF16)
+        nc.vector.memset(ones[:], 1.0)
+        g2be2_rows = consts.tile([P, 2, D], BF16)
+        nc.vector.memset(g2be2_rows[:], 0.0)
+        nc.scalar.dma_start(out=g2be2_rows[0:1, 0, :], in_=g2.rearrange("(o d) -> o d", o=1))
+        nc.scalar.dma_start(out=g2be2_rows[0:1, 1, :], in_=be2.rearrange("(o d) -> o d", o=1))
+        g2be2 = psum_c.tile([P, 2, D], BF16)
         nc.scalar.activation(out=warm[:], in_=warm[:], func=ACT.Gelu)
         b1_bc = consts.tile([P, F], BF16)
         nc.scalar.copy(
@@ -330,14 +336,14 @@ def tile_emaaggregator_pa_t_kernel(
         def centre_times_g2(i):
             scaled = outs.tile([P, D], F32)
             nc.vector.scalar_tensor_tensor(
-                out=scaled[:], in0=y_of[i][:], scalar=mean2_of[i][:], in1=g2_bc[:], op0=ALU.add, op1=ALU.mult
+                out=scaled[:], in0=y_of[i][:], scalar=mean2_of[i][:], in1=g2be2[:, 0, :], op0=ALU.add, op1=ALU.mult
             )
             scaled_of[i] = scaled
 
         def finish(i):
             result = outs.tile([P, D], F32)
             nc.vector.scalar_tensor_tensor(
-                out=result[:], in0=scaled_of[i][:], scalar=rstd2_of[i], in1=be2_bc[:], op0=ALU.mult, op1=ALU.add
+                out=result[:], in0=scaled_of[i][:], scalar=rstd2_of[i], in1=g2be2[:, 1, :], op0=ALU.mult, op1=ALU.add
             )
             nc.sync.dma_start(out=out_rows[:, i, :], in_=result[:])
 
@@ -349,8 +355,8 @@ def tile_emaaggregator_pa_t_kernel(
         for k in range(-4, ROW_TILES + 15):
             if k == 0:
                 nc.scalar.dma_start(out=b2_bc[:], in_=b2.partition_broadcast(P))
-                nc.scalar.dma_start(out=g2_bc[:], in_=g2.partition_broadcast(P))
-                nc.scalar.dma_start(out=be2_bc[:], in_=be2.partition_broadcast(P))
+                for v in range(2):
+                    nc.tensor.matmul(g2be2[:, v, :], lhsT=ones[:], rhs=g2be2_rows[:, v, :], start=True, stop=True)
             when_live(add_b1, k)
             when_live(matmul_1, k + 1)
             when_live(add_b2, k - 11)
@@ -361,6 +367,8 @@ def tile_emaaggregator_pa_t_kernel(
             else:
                 when_live(group_z, k + 3, True)
                 when_live(transpose_z, k + 4)
+            when_live(centre_times_g2, k - 13)
+            when_live(finish, k - 14)
             when_live(group_h, k - 9)
             inv_std(k, k - 3, k - 13)
             when_live(scale_shift_1, k - 7, 0, False)
@@ -378,7 +386,5 @@ def tile_emaaggregator_pa_t_kernel(
             when_live(mean_2, k - 11)
             when_live(var_2, k - 12, k)
             when_live(normalise_1, k - 4)
-            when_live(centre_times_g2, k - 12)
-            when_live(finish, k - 14)
             when_live(quantise_z, k + 2)
             when_live(quantise_h, k - 9)

@@ -226,7 +226,7 @@ def tile_emaaggregator_pa_t_kernel(
 
         def normalise_1(i):
             n = wide.tile([P, F], F32)
-            nc.vector.tensor_scalar(
+            nc.gpsimd.tensor_scalar(
                 out=n[:],
                 in0=x_of[i][:],
                 scalar1=mean1_of[i][:],
@@ -361,23 +361,16 @@ def tile_emaaggregator_pa_t_kernel(
             when_live(matmul_1, k + 1)
             when_live(add_b2, k - 11)
             when_live(matmul_2, k - 10)
-            odd = k % 2 == 1
-            if odd:
-                when_live(scale_shift_1, k - 7, 1, True)
-            else:
-                when_live(group_z, k + 3, True)
-                when_live(transpose_z, k + 4)
+            when_live(scale_shift_1, k - 7, 1, True)
+            when_live(group_z, k + 3, True)
+            when_live(transpose_z, k + 4)
             when_live(centre_times_g2, k - 13)
             when_live(finish, k - 14)
             when_live(group_h, k - 9)
+            when_live(normalise_1, k - 4)
             inv_std(k, k - 3, k - 13)
             when_live(scale_shift_1, k - 7, 0, False)
-            if not odd:
-                when_live(scale_shift_1, k - 7, 1, False)
             when_live(transpose_n, k - 6)
-            if odd:
-                when_live(group_z, k + 3, False)
-                when_live(transpose_z, k + 4)
             when_live(gelu, k - 1)
             when_live(moments_1, k - 2)
             when_live(mean_1, k - 1)
@@ -385,6 +378,5 @@ def tile_emaaggregator_pa_t_kernel(
             when_live(var_1, k - 2, k)
             when_live(mean_2, k - 11)
             when_live(var_2, k - 12, k)
-            when_live(normalise_1, k - 4)
             when_live(quantise_z, k + 2)
             when_live(quantise_h, k - 9)

@@ -224,9 +224,10 @@ def tile_emaaggregator_pa_t_kernel(
             rstd1_of[i1] = rstd[:, 0:1]
             rstd2_of[i2] = rstd[:, 1:2]
 
-        def normalise_1(i):
+        def normalise_1(i, on_vector):
             n = wide.tile([P, F], F32)
-            nc.gpsimd.tensor_scalar(
+            engine = nc.vector if on_vector else nc.gpsimd
+            engine.tensor_scalar(
                 out=n[:],
                 in0=x_of[i][:],
                 scalar1=mean1_of[i][:],
@@ -361,15 +362,24 @@ def tile_emaaggregator_pa_t_kernel(
             when_live(matmul_1, k + 1)
             when_live(add_b2, k - 11)
             when_live(matmul_2, k - 10)
-            when_live(scale_shift_1, k - 7, 1, True)
+            vector_shares = k < ROW_TILES
+            vector_takes_both = k < 11
+            if vector_shares:
+                when_live(scale_shift_1, k - 7, 1, True)
+            if vector_takes_both:
+                when_live(scale_shift_1, k - 7, 0, True)
             when_live(group_z, k + 3, True)
             when_live(transpose_z, k + 4)
             when_live(centre_times_g2, k - 13)
             when_live(finish, k - 14)
             when_live(group_h, k - 9)
-            when_live(normalise_1, k - 4)
+            if vector_shares:
+                when_live(normalise_1, k - 4, False)
             inv_std(k, k - 3, k - 13)
-            when_live(scale_shift_1, k - 7, 0, False)
+            if not vector_takes_both:
+                when_live(scale_shift_1, k - 7, 0, False)
+            if not vector_shares:
+                when_live(scale_shift_1, k - 7, 1, False)
             when_live(transpose_n, k - 6)
             when_live(gelu, k - 1)
             when_live(moments_1, k - 2)
@@ -378,5 +388,7 @@ def tile_emaaggregator_pa_t_kernel(
             when_live(var_1, k - 2, k)
             when_live(mean_2, k - 11)
             when_live(var_2, k - 12, k)
-            when_live(quantise_z, k + 2)
+            if not vector_shares:
+                when_live(normalise_1, k - 4, True)
             when_live(quantise_h, k - 9)
+            when_live(quantise_z, k + 2)

@@ -61,7 +61,7 @@ def tile_emaaggregator_pa_t_kernel(
         make_identity(nc, ident[:])
 
         z_sb = consts.tile([P, ROW_TILES, D], BF16)
-        nc.sync.dma_start(out=z_sb[:, 0:1, :], in_=z_rows[:, 0:1, :])
+        nc.scalar.dma_start(out=z_sb[:, 0:2, :], in_=z_rows[:, 0:2, :])
         w1_words_raw = consts.tile([P, F], U32, align_bytes=64)
         nc.sync.dma_start(
             out=w1_words_raw[:].bitcast(I32),
@@ -81,7 +81,7 @@ def tile_emaaggregator_pa_t_kernel(
             out=w1_scales[:].rearrange("p (g t m) -> p g t m", g=F_PASSES, t=PACK),
             in_=w1_scales_raw[:].rearrange("p (g m t) -> p g t m", g=F_PASSES, t=PACK),
         )
-        nc.sync.dma_start(out=z_sb[:, 1:Z_CHUNK, :], in_=z_rows[:, 1:Z_CHUNK, :])
+        nc.sync.dma_start(out=z_sb[:, 2:Z_CHUNK, :], in_=z_rows[:, 2:Z_CHUNK, :])
         w2_words = consts.tile([P, F_PASSES, D], U32, align_bytes=64)
         for g in range(F_PASSES):
             nc.sync.dma_start(
@@ -118,9 +118,7 @@ def tile_emaaggregator_pa_t_kernel(
             in_=b1_raw[:].rearrange("p (g m t) -> p g t m", g=F_PASSES, t=PACK),
         )
         g1_col = consts.tile([P, F_PASSES * PACK], F32)
-        nc.vector.tensor_copy(out=g1_col[:], in_=g1_raw[:].rearrange("p g t -> p (g t)"))
         be1_col = consts.tile([P, F_PASSES * PACK], F32)
-        nc.vector.tensor_copy(out=be1_col[:], in_=be1_raw[:].rearrange("p g t -> p (g t)"))
 
         junk = consts.tile([P, F], BF16)
 
@@ -356,6 +354,10 @@ def tile_emaaggregator_pa_t_kernel(
         for k in range(-4, ROW_TILES + 15):
             if k == 0:
                 nc.scalar.dma_start(out=b2_bc[:], in_=b2.partition_broadcast(P))
+            if k == 5:
+                nc.vector.tensor_copy(out=g1_col[:], in_=g1_raw[:].rearrange("p g t -> p (g t)"))
+                nc.vector.tensor_copy(out=be1_col[:], in_=be1_raw[:].rearrange("p g t -> p (g t)"))
+            if k == 8:
                 for v in range(2):
                     nc.tensor.matmul(g2be2[:, v, :], lhsT=ones[:], rhs=g2be2_rows[:, v, :], start=True, stop=True)
             when_live(add_b1, k)

@@ -50,10 +50,9 @@ def tile_emaaggregator_pa_t_kernel(
 
         warm = consts.tile([P, 1], F32)
         nc.vector.memset(warm[:], 0.0)
-        w1_scales_raw = consts.tile([P, F], U8, align_bytes=64)
         w1_scales = consts.tile([P, F], U8, align_bytes=64)
         w2_scales = consts.tile([P, F_PASSES, D], U8, align_bytes=64)
-        nc.vector.memset(w1_scales_raw[:].bitcast(I32), 0)
+        nc.vector.memset(w1_scales[:].bitcast(I32), 0)
         nc.vector.memset(w2_scales[:].bitcast(I32), 0)
         neg_half = consts.tile([P, 2], F32)
         nc.vector.memset(neg_half[:], -0.5)
@@ -62,25 +61,16 @@ def tile_emaaggregator_pa_t_kernel(
 
         z_sb = consts.tile([P, ROW_TILES, D], BF16)
         nc.scalar.dma_start(out=z_sb[:, 0:2, :], in_=z_rows[:, 0:2, :])
-        w1_words_raw = consts.tile([P, F], U32, align_bytes=64)
+        w1_words = consts.tile([P, F], U32, align_bytes=64)
         nc.sync.dma_start(
-            out=w1_words_raw[:].bitcast(I32),
+            out=w1_words[:].bitcast(I32),
             in_=W1_words[0].rearrange("p n t -> p (n t)").bitcast(I32),
         )
         for q in range(4):
             nc.sync.dma_start(
-                out=w1_scales_raw[32 * q : 32 * q + 4, :].bitcast(I32),
+                out=w1_scales[32 * q : 32 * q + 4, :].bitcast(I32),
                 in_=W1_scales[0, 4 * q : 4 * q + 4, :].bitcast(I32),
             )
-        w1_words = consts.tile([P, F], U32, align_bytes=64)
-        nc.vector.tensor_copy(
-            out=w1_words[:].bitcast(I32).rearrange("p (g t m) -> p g t m", g=F_PASSES, t=PACK),
-            in_=w1_words_raw[:].bitcast(I32).rearrange("p (g m t) -> p g t m", g=F_PASSES, t=PACK),
-        )
-        nc.vector.tensor_copy(
-            out=w1_scales[:].rearrange("p (g t m) -> p g t m", g=F_PASSES, t=PACK),
-            in_=w1_scales_raw[:].rearrange("p (g m t) -> p g t m", g=F_PASSES, t=PACK),
-        )
         nc.sync.dma_start(out=z_sb[:, 2:Z_CHUNK, :], in_=z_rows[:, 2:Z_CHUNK, :])
         w2_words = consts.tile([P, F_PASSES, D], U32, align_bytes=64)
         for g in range(F_PASSES):
@@ -173,7 +163,12 @@ def tile_emaaggregator_pa_t_kernel(
             x = wide.tile([P, F], F32)
             for g in range(F_PASSES):
                 cols = slice(g * K_PASS, (g + 1) * K_PASS)
-                nc.vector.tensor_tensor(out=x[:, cols], in0=acc1_of[i][g][:], in1=b1_bc[:, cols], op=ALU.add)
+                nc.vector.tensor_tensor(
+                    out=x[:, cols].rearrange("p (t m) -> p t m", t=PACK),
+                    in0=acc1_of[i][g][:].rearrange("p (m t) -> p t m", t=PACK),
+                    in1=b1_bc[:, cols].rearrange("p (t m) -> p t m", t=PACK),
+                    op=ALU.add,
+                )
             x_of[i] = x
 
         def gelu(i):

@@ -48,69 +48,97 @@ def tile_emaaggregator_pa_t_kernel(
         z_rows = z.rearrange("(p i) k -> p i k", i=ROW_TILES)
         out_rows = out.rearrange("(p i) d -> p i d", i=ROW_TILES)
 
+        ctx.enter_context(tc.manual_schedule())
+
+        w1_scales = consts.tile([P, F], U8, align_bytes=64)
+        nc.vector.memset(w1_scales[:].bitcast(I32), 0)
+        b1_row = consts.tile([P, F], BF16)
+        nc.vector.memset(b1_row[:].bitcast(F32), 0.0)
         warm = consts.tile([P, 1], F32)
         nc.vector.memset(warm[:], 0.0)
-        w1_scales = consts.tile([P, F], U8, align_bytes=64)
+        ones = consts.tile([P, P], BF16)
+        nc.vector.memset(ones[:], 1.0)
+        ident = consts.tile([P, P], F32)
+        make_identity(nc, ident[:])
+        b2g2be2_row = consts.tile([P, 3, D], BF16)
+        nc.gpsimd.memset(b2g2be2_row[:].bitcast(F32), 0.0)
         w2_scales = consts.tile([P, F_PASSES, D], U8, align_bytes=64)
-        nc.vector.memset(w1_scales[:].bitcast(I32), 0)
         nc.vector.memset(w2_scales[:].bitcast(I32), 0)
         neg_half = consts.tile([P, 2], F32)
         nc.vector.memset(neg_half[:], -0.5)
-        ident = consts.tile([P, P], F32)
-        make_identity(nc, ident[:])
 
         z_sb = consts.tile([P, ROW_TILES, D], BF16)
         nc.scalar.dma_start(out=z_sb[:, 0:2, :], in_=z_rows[:, 0:2, :])
-        w1_words = consts.tile([P, F], U32, align_bytes=64)
-        nc.sync.dma_start(
-            out=w1_words[:].bitcast(I32),
-            in_=W1_words[0].rearrange("p n t -> p (n t)").bitcast(I32),
-        )
+        nc.scalar.dma_start(out=b1_row[0:1, :], in_=b1.rearrange("(o f) -> o f", o=1))
         for q in range(4):
             nc.sync.dma_start(
                 out=w1_scales[32 * q : 32 * q + 4, :].bitcast(I32),
                 in_=W1_scales[0, 4 * q : 4 * q + 4, :].bitcast(I32),
             )
+        w1_words = consts.tile([P, F], U32, align_bytes=64)
+        nc.sync.dma_start(
+            out=w1_words[:].bitcast(I32),
+            in_=W1_words[0].rearrange("p n t -> p (n t)").bitcast(I32),
+        )
         nc.sync.dma_start(out=z_sb[:, 2:Z_CHUNK, :], in_=z_rows[:, 2:Z_CHUNK, :])
+        nc.sync.dma_start(out=z_sb[:, Z_CHUNK : 2 * Z_CHUNK, :], in_=z_rows[:, Z_CHUNK : 2 * Z_CHUNK, :])
         w2_words = consts.tile([P, F_PASSES, D], U32, align_bytes=64)
         for g in range(F_PASSES):
-            nc.sync.dma_start(
-                out=w2_words[:, g, :].bitcast(I32),
-                in_=W2_words[g].rearrange("p n t -> p (n t)").bitcast(I32),
-            )
             for q in range(4):
                 nc.sync.dma_start(
                     out=w2_scales[32 * q : 32 * q + 4, g, :].bitcast(I32),
                     in_=W2_scales[g, 4 * q : 4 * q + 4, :].bitcast(I32),
                 )
-        for c in range(1, ROW_TILES // Z_CHUNK):
+        for g in range(F_PASSES):
+            nc.sync.dma_start(
+                out=w2_words[:, g, :].bitcast(I32),
+                in_=W2_words[g].rearrange("p n t -> p (n t)").bitcast(I32),
+            )
+        for c in range(2, ROW_TILES // Z_CHUNK):
             rows = slice(c * Z_CHUNK, (c + 1) * Z_CHUNK)
             nc.sync.dma_start(out=z_sb[:, rows, :], in_=z_rows[:, rows, :])
 
-        b1_raw = consts.tile([P, F], BF16)
-        nc.scalar.dma_start(out=b1_raw[:], in_=b1.partition_broadcast(P))
-        g1_raw = consts.tile([P, F_PASSES, PACK], BF16)
-        nc.scalar.dma_start(out=g1_raw[:], in_=g1.rearrange("(g p t) -> p g t", g=F_PASSES, t=PACK))
-        be1_raw = consts.tile([P, F_PASSES, PACK], BF16)
-        nc.scalar.dma_start(out=be1_raw[:], in_=be1.rearrange("(g p t) -> p g t", g=F_PASSES, t=PACK))
-        b2_bc = consts.tile([P, D], BF16)
-        ones = consts.tile([P, P], BF16)
-        nc.vector.memset(ones[:], 1.0)
-        g2be2_rows = consts.tile([P, 2, D], BF16)
-        nc.vector.memset(g2be2_rows[:], 0.0)
-        nc.scalar.dma_start(out=g2be2_rows[0:1, 0, :], in_=g2.rearrange("(o d) -> o d", o=1))
-        nc.scalar.dma_start(out=g2be2_rows[0:1, 1, :], in_=be2.rearrange("(o d) -> o d", o=1))
-        g2be2 = psum_c.tile([P, 2, D], BF16)
         nc.scalar.activation(out=warm[:], in_=warm[:], func=ACT.Gelu)
+        g1_raw = consts.tile([P, F_PASSES, PACK], BF16)
+        be1_raw = consts.tile([P, F_PASSES, PACK], BF16)
+
         b1_bc = consts.tile([P, F], BF16)
-        nc.scalar.copy(
-            out=b1_bc[:].rearrange("p (g t m) -> p g t m", g=F_PASSES, t=PACK),
-            in_=b1_raw[:].rearrange("p (g m t) -> p g t m", g=F_PASSES, t=PACK),
-        )
+        b2_bc = consts.tile([P, D], BF16)
+        g2be2 = psum_c.tile([P, 2, D], BF16)
         g1_col = consts.tile([P, F_PASSES * PACK], F32)
         be1_col = consts.tile([P, F_PASSES * PACK], F32)
 
         junk = consts.tile([P, F], BF16)
+
+        def spread(row):
+            acc = psum_y.tile([P, D], F32)
+            nc.tensor.matmul(acc[:], lhsT=ones[:], rhs=row, start=True, stop=True)
+            return acc
+
+        def spread_b1():
+            for g in range(F_PASSES):
+                cols = slice(g * K_PASS, (g + 1) * K_PASS)
+                acc = spread(b1_row[:, cols])
+                nc.scalar.copy(
+                    out=b1_bc[:, cols].rearrange("p (t m) -> p t m", t=PACK),
+                    in_=acc[:].rearrange("p (m t) -> p t m", t=PACK),
+                )
+
+        def load_small_vectors():
+            nc.scalar.dma_start(out=g1_raw[:], in_=g1.rearrange("(g p t) -> p g t", g=F_PASSES, t=PACK))
+            nc.scalar.dma_start(out=be1_raw[:], in_=be1.rearrange("(g p t) -> p g t", g=F_PASSES, t=PACK))
+            for v, vector in enumerate((b2, g2, be2)):
+                nc.scalar.dma_start(out=b2g2be2_row[0:1, v, :], in_=vector.rearrange("(o d) -> o d", o=1))
+
+        def spread_b2_g2_be2():
+            acc = spread(b2g2be2_row[:, 0, :])
+            nc.scalar.copy(out=b2_bc[:], in_=acc[:])
+            for v in range(2):
+                nc.tensor.matmul(g2be2[:, v, :], lhsT=ones[:], rhs=b2g2be2_row[:, v + 1, :], start=True, stop=True)
+
+        def cast_g1_be1():
+            nc.vector.tensor_copy(out=g1_col[:], in_=g1_raw[:].rearrange("p g t -> p (g t)"))
+            nc.vector.tensor_copy(out=be1_col[:], in_=be1_raw[:].rearrange("p g t -> p (g t)"))
 
         sum1_of, sum2_of, ve_of = {}, {}, {}
         zt_of, zg_of, zq_of, acc1_of, x_of, mean1_of, sq1_of, rstd1_of, n_of = {}, {}, {}, {}, {}, {}, {}, {}, {}
@@ -345,16 +373,14 @@ def tile_emaaggregator_pa_t_kernel(
             if 0 <= i < ROW_TILES:
                 stage(i, *more)
 
-        ctx.enter_context(tc.manual_schedule())
-        for k in range(-4, ROW_TILES + 15):
-            if k == 0:
-                nc.scalar.dma_start(out=b2_bc[:], in_=b2.partition_broadcast(P))
+        for k in range(-3, ROW_TILES + 15):
+            if k == -2:
+                spread_b1()
+                load_small_vectors()
             if k == 5:
-                nc.vector.tensor_copy(out=g1_col[:], in_=g1_raw[:].rearrange("p g t -> p (g t)"))
-                nc.vector.tensor_copy(out=be1_col[:], in_=be1_raw[:].rearrange("p g t -> p (g t)"))
-            if k == 8:
-                for v in range(2):
-                    nc.tensor.matmul(g2be2[:, v, :], lhsT=ones[:], rhs=g2be2_rows[:, v, :], start=True, stop=True)
+                cast_g1_be1()
+            if k == 6:
+                spread_b2_g2_be2()
             when_live(add_b1, k)
             when_live(matmul_1, k + 1)
             when_live(add_b2, k - 11)
@@ -365,8 +391,8 @@ def tile_emaaggregator_pa_t_kernel(
                 when_live(scale_shift_1, k - 7, 1, True)
             if vector_takes_both:
                 when_live(scale_shift_1, k - 7, 0, True)
-            when_live(group_z, k + 3, True)
-            when_live(transpose_z, k + 4)
+            when_live(group_z, k + 2, True)
+            when_live(transpose_z, k + 3)
             when_live(centre_times_g2, k - 13)
             when_live(finish, k - 14)
             when_live(group_h, k - 9)

@@ -241,7 +241,7 @@ def tile_emaaggregator_pa_t_kernel(
                 return
             cols = slice(0 if live1 else 1, 2 if live2 else 1)
             rstd = stats.tile([P, 2], F32)
-            nc.gpsimd.tensor_tensor(out=rstd[:, cols], in0=ve_of[k - 1][:, cols], in1=neg_half[:, cols], op=ALU.pow)
+            nc.gpsimd.tensor_tensor(out=rstd[:, cols], in0=ve_of[k][:, cols], in1=neg_half[:, cols], op=ALU.pow)
             rstd1_of[i1] = rstd[:, 0:1]
             rstd2_of[i2] = rstd[:, 1:2]
 
@@ -377,41 +377,42 @@ def tile_emaaggregator_pa_t_kernel(
             if k == -2:
                 spread_b1()
                 load_small_vectors()
-            if k == 5:
-                cast_g1_be1()
-            if k == 6:
+            if k == 2:
                 spread_b2_g2_be2()
+            if k == 3:
+                cast_g1_be1()
             when_live(add_b1, k)
             when_live(matmul_1, k + 1)
             when_live(add_b2, k - 11)
             when_live(matmul_2, k - 10)
-            vector_shares = k < ROW_TILES
-            vector_takes_both = k < 11
+            vector_shares = k < ROW_TILES + 2
+            vector_takes_both = k < 9
+            vector_normalises = k > ROW_TILES
             if vector_shares:
                 when_live(scale_shift_1, k - 7, 1, True)
             if vector_takes_both:
                 when_live(scale_shift_1, k - 7, 0, True)
-            when_live(group_z, k + 2, True)
+            when_live(group_z, k + 2, not (k > 10 and k % 2))
             when_live(transpose_z, k + 3)
             when_live(centre_times_g2, k - 13)
             when_live(finish, k - 14)
             when_live(group_h, k - 9)
-            if vector_shares:
+            if not vector_normalises:
                 when_live(normalise_1, k - 4, False)
-            inv_std(k, k - 3, k - 13)
             if not vector_takes_both:
                 when_live(scale_shift_1, k - 7, 0, False)
             if not vector_shares:
                 when_live(scale_shift_1, k - 7, 1, False)
             when_live(transpose_n, k - 6)
             when_live(gelu, k - 1)
+            when_live(var_1, k - 3, k)
+            when_live(var_2, k - 13, k)
+            inv_std(k, k - 3, k - 13)
             when_live(moments_1, k - 2)
             when_live(mean_1, k - 1)
             when_live(moments_2, k - 12)
-            when_live(var_1, k - 2, k)
             when_live(mean_2, k - 11)
-            when_live(var_2, k - 12, k)
-            if not vector_shares:
+            if vector_normalises:
                 when_live(normalise_1, k - 4, True)
             when_live(quantise_h, k - 9)
             when_live(quantise_z, k + 2)

@@ -68,18 +68,21 @@ def tile_emaaggregator_pa_t_kernel(
         nc.vector.memset(neg_half[:], -0.5)
 
         z_sb = consts.tile([P, ROW_TILES, D], BF16)
-        nc.scalar.dma_start(out=z_sb[:, 0:2, :], in_=z_rows[:, 0:2, :])
+        nc.scalar.dma_start(out=z_sb[:, 0:1, :], in_=z_rows[:, 0:1, :])
         nc.scalar.dma_start(out=b1_row[0:1, :], in_=b1.rearrange("(o f) -> o f", o=1))
+        nc.scalar.dma_start(out=z_sb[:, 1:2, :], in_=z_rows[:, 1:2, :])
         for q in range(4):
             nc.sync.dma_start(
                 out=w1_scales[32 * q : 32 * q + 4, :].bitcast(I32),
                 in_=W1_scales[0, 4 * q : 4 * q + 4, :].bitcast(I32),
             )
         w1_words = consts.tile([P, F], U32, align_bytes=64)
-        nc.sync.dma_start(
-            out=w1_words[:].bitcast(I32),
-            in_=W1_words[0].rearrange("p n t -> p (n t)").bitcast(I32),
-        )
+        for g in range(F_PASSES):
+            cols = slice(g * K_PASS, (g + 1) * K_PASS)
+            nc.sync.dma_start(
+                out=w1_words[:, cols].bitcast(I32),
+                in_=W1_words[0, :, cols, :].rearrange("p n t -> p (n t)").bitcast(I32),
+            )
         nc.sync.dma_start(out=z_sb[:, 2:Z_CHUNK, :], in_=z_rows[:, 2:Z_CHUNK, :])
         nc.sync.dma_start(out=z_sb[:, Z_CHUNK : 2 * Z_CHUNK, :], in_=z_rows[:, Z_CHUNK : 2 * Z_CHUNK, :])
         w2_words = consts.tile([P, F_PASSES, D], U32, align_bytes=64)
@@ -373,46 +376,49 @@ def tile_emaaggregator_pa_t_kernel(
             if 0 <= i < ROW_TILES:
                 stage(i, *more)
 
-        for k in range(-3, ROW_TILES + 15):
+        for k in range(-3, ROW_TILES + 13):
             if k == -2:
                 spread_b1()
                 load_small_vectors()
-            if k == 2:
-                spread_b2_g2_be2()
-            if k == 3:
+            if k == 1:
                 cast_g1_be1()
-            when_live(add_b1, k)
-            when_live(matmul_1, k + 1)
-            when_live(add_b2, k - 11)
-            when_live(matmul_2, k - 10)
-            vector_shares = k < ROW_TILES + 2
-            vector_takes_both = k < 9
+            if k == 5:
+                spread_b2_g2_be2()
+            vector_shares = k < ROW_TILES + 1
+            vector_takes_both = k < 8
             vector_normalises = k > ROW_TILES
+            when_live(add_b1, k)
+            if k == 0:
+                quantise_z(1)
+            when_live(matmul_1, k + 1)
+            when_live(add_b2, k - 10)
+            when_live(matmul_2, k - 9)
             if vector_shares:
-                when_live(scale_shift_1, k - 7, 1, True)
+                when_live(scale_shift_1, k - 6, 1, True)
             if vector_takes_both:
-                when_live(scale_shift_1, k - 7, 0, True)
-            when_live(group_z, k + 2, not (k > 10 and k % 2))
+                when_live(scale_shift_1, k - 6, 0, True)
+            when_live(group_z, k + 2, not (k > 10 and k % 3))
             when_live(transpose_z, k + 3)
-            when_live(centre_times_g2, k - 13)
-            when_live(finish, k - 14)
-            when_live(group_h, k - 9)
+            when_live(centre_times_g2, k - 11)
+            when_live(finish, k - 12)
+            when_live(group_h, k - 8)
             if not vector_normalises:
                 when_live(normalise_1, k - 4, False)
             if not vector_takes_both:
-                when_live(scale_shift_1, k - 7, 0, False)
+                when_live(scale_shift_1, k - 6, 0, False)
             if not vector_shares:
-                when_live(scale_shift_1, k - 7, 1, False)
-            when_live(transpose_n, k - 6)
+                when_live(scale_shift_1, k - 6, 1, False)
             when_live(gelu, k - 1)
+            when_live(mean_2, k - 10)
             when_live(var_1, k - 3, k)
-            when_live(var_2, k - 13, k)
-            inv_std(k, k - 3, k - 13)
+            when_live(var_2, k - 11, k)
+            inv_std(k, k - 3, k - 11)
             when_live(moments_1, k - 2)
             when_live(mean_1, k - 1)
-            when_live(moments_2, k - 12)
-            when_live(mean_2, k - 11)
+            when_live(moments_2, k - 10)
             if vector_normalises:
                 when_live(normalise_1, k - 4, True)
-            when_live(quantise_h, k - 9)
-            when_live(quantise_z, k + 2)
+            when_live(transpose_n, k - 5)
+            when_live(quantise_h, k - 8)
+            if k != -1:
+                when_live(quantise_z, k + 2)

@@ -85,6 +85,13 @@ def tile_emaaggregator_pa_t_kernel(
             )
         nc.sync.dma_start(out=z_sb[:, 2:Z_CHUNK, :], in_=z_rows[:, 2:Z_CHUNK, :])
         nc.sync.dma_start(out=z_sb[:, Z_CHUNK : 2 * Z_CHUNK, :], in_=z_rows[:, Z_CHUNK : 2 * Z_CHUNK, :])
+        g1_raw = consts.tile([P, F_PASSES, PACK], BF16)
+        nc.sync.dma_start(out=g1_raw[:], in_=g1.rearrange("(g p t) -> p g t", g=F_PASSES, t=PACK))
+        be1_raw = consts.tile([P, F_PASSES, PACK], BF16)
+        nc.sync.dma_start(out=be1_raw[:], in_=be1.rearrange("(g p t) -> p g t", g=F_PASSES, t=PACK))
+        for v, vector in enumerate((b2, g2, be2)):
+            nc.sync.dma_start(out=b2g2be2_row[0:1, v, :], in_=vector.rearrange("(o d) -> o d", o=1))
+        nc.sync.dma_start(out=z_sb[:, 2 * Z_CHUNK : 3 * Z_CHUNK, :], in_=z_rows[:, 2 * Z_CHUNK : 3 * Z_CHUNK, :])
         w2_words = consts.tile([P, F_PASSES, D], U32, align_bytes=64)
         for g in range(F_PASSES):
             for q in range(4):
@@ -97,13 +104,11 @@ def tile_emaaggregator_pa_t_kernel(
                 out=w2_words[:, g, :].bitcast(I32),
                 in_=W2_words[g].rearrange("p n t -> p (n t)").bitcast(I32),
             )
-        for c in range(2, ROW_TILES // Z_CHUNK):
+        for c in range(3, ROW_TILES // Z_CHUNK):
             rows = slice(c * Z_CHUNK, (c + 1) * Z_CHUNK)
             nc.sync.dma_start(out=z_sb[:, rows, :], in_=z_rows[:, rows, :])
 
         nc.scalar.activation(out=warm[:], in_=warm[:], func=ACT.Gelu)
-        g1_raw = consts.tile([P, F_PASSES, PACK], BF16)
-        be1_raw = consts.tile([P, F_PASSES, PACK], BF16)
 
         b1_bc = consts.tile([P, F], BF16)
         b2_bc = consts.tile([P, D], BF16)
@@ -127,12 +132,6 @@ def tile_emaaggregator_pa_t_kernel(
                     in_=acc[:].rearrange("p (m t) -> p t m", t=PACK),
                 )
 
-        def load_small_vectors():
-            nc.scalar.dma_start(out=g1_raw[:], in_=g1.rearrange("(g p t) -> p g t", g=F_PASSES, t=PACK))
-            nc.scalar.dma_start(out=be1_raw[:], in_=be1.rearrange("(g p t) -> p g t", g=F_PASSES, t=PACK))
-            for v, vector in enumerate((b2, g2, be2)):
-                nc.scalar.dma_start(out=b2g2be2_row[0:1, v, :], in_=vector.rearrange("(o d) -> o d", o=1))
-
         def spread_b2_g2_be2():
             acc = spread(b2g2be2_row[:, 0, :])
             nc.scalar.copy(out=b2_bc[:], in_=acc[:])
@@ -140,8 +139,8 @@ def tile_emaaggregator_pa_t_kernel(
                 nc.tensor.matmul(g2be2[:, v, :], lhsT=ones[:], rhs=b2g2be2_row[:, v + 1, :], start=True, stop=True)
 
         def cast_g1_be1():
-            nc.vector.tensor_copy(out=g1_col[:], in_=g1_raw[:].rearrange("p g t -> p (g t)"))
-            nc.vector.tensor_copy(out=be1_col[:], in_=be1_raw[:].rearrange("p g t -> p (g t)"))
+            nc.scalar.copy(out=g1_col[:], in_=g1_raw[:].rearrange("p g t -> p (g t)"))
+            nc.scalar.copy(out=be1_col[:], in_=be1_raw[:].rearrange("p g t -> p (g t)"))
 
         sum1_of, sum2_of, ve_of = {}, {}, {}
         zt_of, zg_of, zq_of, acc1_of, x_of, mean1_of, sq1_of, rstd1_of, n_of = {}, {}, {}, {}, {}, {}, {}, {}, {}
@@ -379,46 +378,46 @@ def tile_emaaggregator_pa_t_kernel(
         for k in range(-3, ROW_TILES + 13):
             if k == -2:
                 spread_b1()
-                load_small_vectors()
-            if k == 1:
+            if k == 4:
                 cast_g1_be1()
             if k == 5:
                 spread_b2_g2_be2()
-            vector_shares = k < ROW_TILES + 1
-            vector_takes_both = k < 8
+            vector_shares = k < ROW_TILES + 2
+            vector_takes_both = k < 10
             vector_normalises = k > ROW_TILES
+            vector_groups_z = k < 11 or k % 4 == 0
+            when_live(matmul_2, k - 9)
+            when_live(add_b2, k - 10)
             when_live(add_b1, k)
             if k == 0:
                 quantise_z(1)
             when_live(matmul_1, k + 1)
-            when_live(add_b2, k - 10)
-            when_live(matmul_2, k - 9)
-            if vector_shares:
-                when_live(scale_shift_1, k - 6, 1, True)
-            if vector_takes_both:
-                when_live(scale_shift_1, k - 6, 0, True)
-            when_live(group_z, k + 2, not (k > 10 and k % 3))
+            when_live(group_z, k + 2, vector_groups_z)
             when_live(transpose_z, k + 3)
             when_live(centre_times_g2, k - 11)
             when_live(finish, k - 12)
+            if vector_takes_both:
+                when_live(scale_shift_1, k - 6, 0, True)
+            if vector_shares:
+                when_live(scale_shift_1, k - 6, 1, True)
             when_live(group_h, k - 8)
             if not vector_normalises:
                 when_live(normalise_1, k - 4, False)
-            if not vector_takes_both:
-                when_live(scale_shift_1, k - 6, 0, False)
-            if not vector_shares:
-                when_live(scale_shift_1, k - 6, 1, False)
             when_live(gelu, k - 1)
-            when_live(mean_2, k - 10)
             when_live(var_1, k - 3, k)
             when_live(var_2, k - 11, k)
             inv_std(k, k - 3, k - 11)
+            if not vector_takes_both:
+                when_live(scale_shift_1, k - 6, 0, False)
+            when_live(mean_2, k - 10)
+            if not vector_shares:
+                when_live(scale_shift_1, k - 6, 1, False)
             when_live(moments_1, k - 2)
             when_live(mean_1, k - 1)
             when_live(moments_2, k - 10)
+            when_live(quantise_h, k - 8)
             if vector_normalises:
                 when_live(normalise_1, k - 4, True)
             when_live(transpose_n, k - 5)
-            when_live(quantise_h, k - 8)
             if k != -1:
                 when_live(quantise_z, k + 2)

from contextlib import ExitStack

import concourse.mybir as mybir
from concourse.masks import make_identity

FLOPS = 2 * 4096 * 512 * 1024 * 2

F32 = mybir.dt.float32
BF16 = mybir.dt.bfloat16
I32 = mybir.dt.int32
U32 = mybir.dt.uint32
U8 = mybir.dt.uint8
FP8X4 = mybir.dt.float8_e4m3fn_x4
ALU = mybir.AluOpType
ACT = mybir.ActivationFunctionType

P = 128
PACK = 4
K_PASS = P * PACK
ROWS = 4096
D = 512
F = 1024
F_PASSES = F // K_PASS
ROW_TILES = ROWS // P
Z_CHUNK = 4
EPS = 1e-5


def tile_emaaggregator_pa_t_kernel(
    tc, z, W1_words, W1_scales, b1, g1, be1, W2_words, W2_scales, b2, g2, be2, out
):
    nc = tc.nc
    with ExitStack() as ctx:
        consts = ctx.enter_context(tc.tile_pool(name="consts", bufs=1))
        zq_pool = ctx.enter_context(tc.tile_pool(name="zq", bufs=4))
        wide = ctx.enter_context(tc.tile_pool(name="wide", bufs=6))
        plane_pool = ctx.enter_context(tc.tile_pool(name="planes", bufs=3))
        hq_pool = ctx.enter_context(tc.tile_pool(name="hq", bufs=3))
        hg_pool = ctx.enter_context(tc.tile_pool(name="hg", bufs=1))
        outs = ctx.enter_context(tc.tile_pool(name="outs", bufs=4))
        stats = ctx.enter_context(tc.tile_pool(name="stats", bufs=12))
        psum_z = ctx.enter_context(tc.psum_pool(name="psum_z", bufs=1))
        psum_s1 = ctx.enter_context(tc.psum_pool(name="psum_s1", bufs=2))
        psum_c = ctx.enter_context(tc.psum_pool(name="psum_c", bufs=1))
        psum_ht = ctx.enter_context(tc.psum_pool(name="psum_ht", bufs=2))
        psum_y = ctx.enter_context(tc.psum_pool(name="psum_y", bufs=2))

        z_rows = z.rearrange("(p i) k -> p i k", i=ROW_TILES)
        out_rows = out.rearrange("(p i) d -> p i d", i=ROW_TILES)

        ctx.enter_context(tc.manual_schedule())

        w1_scales = consts.tile([P, F], U8, align_bytes=64)
        nc.vector.memset(w1_scales[:].bitcast(I32), 0)
        b1_row = consts.tile([P, F], BF16)
        nc.vector.memset(b1_row[:].bitcast(F32), 0.0)
        warm = consts.tile([P, 1], F32)
        nc.vector.memset(warm[:], 0.0)
        ones = consts.tile([P, P], BF16)
        nc.vector.memset(ones[:], 1.0)
        ident = consts.tile([P, P], F32)
        make_identity(nc, ident[:])
        b2g2be2_row = consts.tile([P, 3, D], BF16)
        nc.gpsimd.memset(b2g2be2_row[:].bitcast(F32), 0.0)
        w2_scales = consts.tile([P, F_PASSES, D], U8, align_bytes=64)
        nc.vector.memset(w2_scales[:].bitcast(I32), 0)
        neg_half = consts.tile([P, 2], F32)
        nc.vector.memset(neg_half[:], -0.5)

        z_sb = consts.tile([P, ROW_TILES, D], BF16)
        nc.scalar.dma_start(out=z_sb[:, 0:1, :], in_=z_rows[:, 0:1, :])
        nc.scalar.dma_start(out=b1_row[0:1, :], in_=b1.rearrange("(o f) -> o f", o=1))
        nc.scalar.dma_start(out=z_sb[:, 1:2, :], in_=z_rows[:, 1:2, :])
        for q in range(4):
            nc.sync.dma_start(
                out=w1_scales[32 * q : 32 * q + 4, :].bitcast(I32),
                in_=W1_scales[0, 4 * q : 4 * q + 4, :].bitcast(I32),
            )
        w1_words = consts.tile([P, F], U32, align_bytes=64)
        for g in range(F_PASSES):
            cols = slice(g * K_PASS, (g + 1) * K_PASS)
            nc.sync.dma_start(
                out=w1_words[:, cols].bitcast(I32),
                in_=W1_words[0, :, cols, :].rearrange("p n t -> p (n t)").bitcast(I32),
            )
        nc.sync.dma_start(out=z_sb[:, 2:Z_CHUNK, :], in_=z_rows[:, 2:Z_CHUNK, :])
        nc.sync.dma_start(out=z_sb[:, Z_CHUNK : 2 * Z_CHUNK, :], in_=z_rows[:, Z_CHUNK : 2 * Z_CHUNK, :])
        g1_raw = consts.tile([P, F_PASSES, PACK], BF16)
        nc.sync.dma_start(out=g1_raw[:], in_=g1.rearrange("(g p t) -> p g t", g=F_PASSES, t=PACK))
        be1_raw = consts.tile([P, F_PASSES, PACK], BF16)
        nc.sync.dma_start(out=be1_raw[:], in_=be1.rearrange("(g p t) -> p g t", g=F_PASSES, t=PACK))
        for v, vector in enumerate((b2, g2, be2)):
            nc.sync.dma_start(out=b2g2be2_row[0:1, v, :], in_=vector.rearrange("(o d) -> o d", o=1))
        nc.sync.dma_start(out=z_sb[:, 2 * Z_CHUNK : 3 * Z_CHUNK, :], in_=z_rows[:, 2 * Z_CHUNK : 3 * Z_CHUNK, :])
        w2_words = consts.tile([P, F_PASSES, D], U32, align_bytes=64)
        for g in range(F_PASSES):
            for q in range(4):
                nc.sync.dma_start(
                    out=w2_scales[32 * q : 32 * q + 4, g, :].bitcast(I32),
                    in_=W2_scales[g, 4 * q : 4 * q + 4, :].bitcast(I32),
                )
        for g in range(F_PASSES):
            nc.sync.dma_start(
                out=w2_words[:, g, :].bitcast(I32),
                in_=W2_words[g].rearrange("p n t -> p (n t)").bitcast(I32),
            )
        for c in range(3, ROW_TILES // Z_CHUNK):
            rows = slice(c * Z_CHUNK, (c + 1) * Z_CHUNK)
            nc.sync.dma_start(out=z_sb[:, rows, :], in_=z_rows[:, rows, :])

        nc.scalar.activation(out=warm[:], in_=warm[:], func=ACT.Gelu)

        b1_bc = consts.tile([P, F], BF16)
        b2_bc = consts.tile([P, D], BF16)
        g2be2 = psum_c.tile([P, 2, D], BF16)
        g1_col = consts.tile([P, F_PASSES * PACK], F32)
        be1_col = consts.tile([P, F_PASSES * PACK], F32)

        junk = consts.tile([P, F], BF16)

        def spread(row):
            acc = psum_y.tile([P, D], F32)
            nc.tensor.matmul(acc[:], lhsT=ones[:], rhs=row, start=True, stop=True)
            return acc

        def spread_b1():
            for g in range(F_PASSES):
                cols = slice(g * K_PASS, (g + 1) * K_PASS)
                acc = spread(b1_row[:, cols])
                nc.scalar.copy(
                    out=b1_bc[:, cols].rearrange("p (t m) -> p t m", t=PACK),
                    in_=acc[:].rearrange("p (m t) -> p t m", t=PACK),
                )

        def spread_b2_g2_be2():
            acc = spread(b2g2be2_row[:, 0, :])
            nc.scalar.copy(out=b2_bc[:], in_=acc[:])
            for v in range(2):
                nc.tensor.matmul(g2be2[:, v, :], lhsT=ones[:], rhs=b2g2be2_row[:, v + 1, :], start=True, stop=True)

        def cast_g1_be1():
            nc.scalar.copy(out=g1_col[:], in_=g1_raw[:].rearrange("p g t -> p (g t)"))
            nc.scalar.copy(out=be1_col[:], in_=be1_raw[:].rearrange("p g t -> p (g t)"))

        sum1_of, sum2_of, ve_of = {}, {}, {}
        zt_of, zg_of, zq_of, acc1_of, x_of, mean1_of, sq1_of, rstd1_of, n_of = {}, {}, {}, {}, {}, {}, {}, {}, {}
        ht_of, planes_of, hg_of, hq_of, acc2_of, y_of, mean2_of, sq2_of, rstd2_of, scaled_of = (
            {}, {}, {}, {}, {}, {}, {}, {}, {}, {},
        )

        def transpose_z(i):
            zt = psum_z.tile([P, 2, P], F32)
            words = z_sb[:, i, :].bitcast(F32)
            for u in range(2):
                nc.tensor.transpose(zt[:, u, :], words[:, u : D // 2 : 2], ident[:])
            zt_of[i] = zt

        def group_z(i, on_vector):
            z_grouped = zq_pool.tile([P, P, 2], F32, align_bytes=64)
            if on_vector:
                nc.vector.tensor_copy(out=z_grouped[:], in_=zt_of[i][:].rearrange("p u r -> p r u"))
            else:
                nc.scalar.copy(out=z_grouped[:], in_=zt_of[i][:].rearrange("p u r -> p r u"))
            zg_of[i] = z_grouped

        def quantise_z(i):
            z_words = zq_pool.tile([P, P], U32, align_bytes=64)
            z_scales = zq_pool.tile([P, P], U8, align_bytes=64)
            nc.vector.quantize_mx(
                out=z_words[:].bitcast(FP8X4),
                scales=z_scales[:],
                in_=zg_of[i][:].rearrange("p r u -> p (r u)").bitcast(BF16),
            )
            zq_of[i] = (z_words, z_scales)

        def matmul_1(i):
            z_words, z_scales = zq_of[i]
            acc1_of[i] = []
            for g in range(F_PASSES):
                acc = psum_s1.tile([P, K_PASS], F32)
                nc.tensor.matmul_mx(
                    out=acc[:],
                    lhsT=z_words[:].bitcast(FP8X4),
                    lhsT_scale=z_scales[:],
                    rhs=w1_words[:, g * K_PASS : (g + 1) * K_PASS].bitcast(FP8X4),
                    rhs_scale=w1_scales[:, g * K_PASS : (g + 1) * K_PASS],
                    start=True,
                    stop=True,
                )
                acc1_of[i].append(acc)

        def add_b1(i):
            x = wide.tile([P, F], F32)
            for g in range(F_PASSES):
                cols = slice(g * K_PASS, (g + 1) * K_PASS)
                nc.vector.tensor_tensor(
                    out=x[:, cols].rearrange("p (t m) -> p t m", t=PACK),
                    in0=acc1_of[i][g][:].rearrange("p (m t) -> p t m", t=PACK),
                    in1=b1_bc[:, cols].rearrange("p (t m) -> p t m", t=PACK),
                    op=ALU.add,
                )
            x_of[i] = x

        def gelu(i):
            sum_x = stats.tile([P, 1], F32)
            nc.scalar.activation(out=x_of[i][:], in_=x_of[i][:], func=ACT.Gelu, accum_out=sum_x[:])
            sum1_of[i] = sum_x

        def minus_mean(total, width):
            neg_mean = stats.tile([P, 1], F32)
            nc.scalar.activation(out=neg_mean[:], in_=total[:], func=ACT.Copy, scale=-1.0 / width)
            return neg_mean

        def mean_1(i):
            mean1_of[i] = minus_mean(sum1_of[i], F)

        def moments_1(i):
            sum_sq = stats.tile([P, 1], F32)
            nc.scalar.activation(
                out=junk[:], in_=x_of[i][:], func=ACT.Square, bias=mean1_of[i][:], accum_out=sum_sq[:]
            )
            sq1_of[i] = sum_sq

        def var_eps(k):
            if k not in ve_of:
                ve = stats.tile([P, 2], F32)
                ve_of[k] = ve
            return ve_of[k]

        def var_1(i, k):
            nc.scalar.activation(
                out=var_eps(k)[:, 0:1], in_=sq1_of[i][:], func=ACT.Copy, scale=1.0 / F, bias=EPS
            )

        def var_2(i, k):
            nc.scalar.activation(
                out=var_eps(k)[:, 1:2], in_=sq2_of[i][:], func=ACT.Copy, scale=1.0 / D, bias=EPS
            )

        def inv_std(k, i1, i2):
            live1, live2 = 0 <= i1 < ROW_TILES, 0 <= i2 < ROW_TILES
            if not (live1 or live2):
                return
            cols = slice(0 if live1 else 1, 2 if live2 else 1)
            rstd = stats.tile([P, 2], F32)
            nc.gpsimd.tensor_tensor(out=rstd[:, cols], in0=ve_of[k][:, cols], in1=neg_half[:, cols], op=ALU.pow)
            rstd1_of[i1] = rstd[:, 0:1]
            rstd2_of[i2] = rstd[:, 1:2]

        def normalise_1(i, on_vector):
            n = wide.tile([P, F], F32)
            engine = nc.vector if on_vector else nc.gpsimd
            engine.tensor_scalar(
                out=n[:],
                in0=x_of[i][:],
                scalar1=mean1_of[i][:],
                scalar2=rstd1_of[i],
                op0=ALU.add,
                op1=ALU.mult,
            )
            n_of[i] = n

        def transpose_n(u):
            pair, g = divmod(u, 2)
            ht_of[u] = []
            for half in range(2):
                ht = psum_ht.tile([P, 2, 2, P], F32)
                for tl in range(2):
                    t = 2 * half + tl
                    for j in range(2):
                        nc.tensor.transpose(
                            ht[:, tl, j, :],
                            n_of[2 * pair + j][:, g * K_PASS + t * P : g * K_PASS + (t + 1) * P],
                            ident[:],
                        )
                ht_of[u].append(ht)

        def scale_shift_1(u, half, on_vector):
            pair, g = divmod(u, 2)
            if pair not in planes_of:
                planes = plane_pool.tile([P, F_PASSES, PACK, 2, P], BF16)
                planes_of[pair] = planes
            for tl in range(2):
                t = 2 * half + tl
                col = g * PACK + t
                if not on_vector:
                    nc.scalar.activation(
                        out=planes_of[pair][:, g, t, :, :],
                        in_=ht_of[u][half][:, tl, :, :],
                        func=ACT.Identity,
                        scale=g1_col[:, col : col + 1],
                        bias=be1_col[:, col : col + 1],
                    )
                else:
                    nc.vector.tensor_scalar(
                        out=planes_of[pair][:, g, t, :, :],
                        in0=ht_of[u][half][:, tl, :, :],
                        scalar1=g1_col[:, col : col + 1],
                        scalar2=be1_col[:, col : col + 1],
                        op0=ALU.mult,
                        op1=ALU.add,
                    )

        def group_h(i):
            h_grouped = hg_pool.tile([P, F_PASSES, P, PACK], BF16, align_bytes=64)
            nc.gpsimd.tensor_scalar(
                out=h_grouped[:],
                in0=planes_of[i // 2][:, :, :, i % 2, :].rearrange("p g t r -> p g r t"),
                scalar1=1.0,
                scalar2=0.0,
                op0=ALU.mult,
                op1=ALU.add,
            )
            hg_of[i] = h_grouped

        def quantise_h(i):
            h_words = hq_pool.tile([P, F_PASSES * P], U32, align_bytes=64)
            h_scales = hq_pool.tile([P, F_PASSES * P], U8, align_bytes=64)
            nc.vector.quantize_mx(
                out=h_words[:].bitcast(FP8X4),
                scales=h_scales[:],
                in_=hg_of[i][:].rearrange("p g r t -> p (g r t)"),
            )
            hq_of[i] = (h_words, h_scales)

        def matmul_2(i):
            h_words, h_scales = hq_of[i]
            acc = psum_y.tile([P, D], F32)
            for g in range(F_PASSES):
                nc.tensor.matmul_mx(
                    out=acc[:],
                    lhsT=h_words[:, g * P : (g + 1) * P].bitcast(FP8X4),
                    lhsT_scale=h_scales[:, g * P : (g + 1) * P],
                    rhs=w2_words[:, g, :].bitcast(FP8X4),
                    rhs_scale=w2_scales[:, g, :],
                    start=(g == 0),
                    stop=(g == F_PASSES - 1),
                )
            acc2_of[i] = acc

        def add_b2(i):
            y = outs.tile([P, D], F32)
            sum_y = stats.tile([P, 1], F32)
            nc.vector.scalar_tensor_tensor(
                out=y[:], in0=acc2_of[i][:], scalar=1.0, in1=b2_bc[:], op0=ALU.mult, op1=ALU.add, accum_out=sum_y[:]
            )
            y_of[i] = y
            sum2_of[i] = sum_y

        def mean_2(i):
            mean2_of[i] = minus_mean(sum2_of[i], D)

        def moments_2(i):
            sum_sq2 = stats.tile([P, 1], F32)
            nc.scalar.activation(
                out=junk[:, 0:D], in_=y_of[i][:], func=ACT.Square, bias=mean2_of[i][:], accum_out=sum_sq2[:]
            )
            sq2_of[i] = sum_sq2

        def centre_times_g2(i):
            scaled = outs.tile([P, D], F32)
            nc.vector.scalar_tensor_tensor(
                out=scaled[:], in0=y_of[i][:], scalar=mean2_of[i][:], in1=g2be2[:, 0, :], op0=ALU.add, op1=ALU.mult
            )
            scaled_of[i] = scaled

        def finish(i):
            result = outs.tile([P, D], F32)
            nc.vector.scalar_tensor_tensor(
                out=result[:], in0=scaled_of[i][:], scalar=rstd2_of[i], in1=g2be2[:, 1, :], op0=ALU.mult, op1=ALU.add
            )
            nc.sync.dma_start(out=out_rows[:, i, :], in_=result[:])

        def when_live(stage, i, *more):
            if 0 <= i < ROW_TILES:
                stage(i, *more)

        for k in range(-3, ROW_TILES + 13):
            if k == -2:
                spread_b1()
            if k == 4:
                cast_g1_be1()
            if k == 5:
                spread_b2_g2_be2()
            vector_shares = k < ROW_TILES + 2
            vector_takes_both = k < 10
            vector_normalises = k > ROW_TILES
            vector_groups_z = k < 11 or k % 4 == 0
            when_live(matmul_2, k - 9)
            when_live(add_b2, k - 10)
            when_live(add_b1, k)
            if k == 0:
                quantise_z(1)
            when_live(matmul_1, k + 1)
            when_live(group_z, k + 2, vector_groups_z)
            when_live(transpose_z, k + 3)
            when_live(centre_times_g2, k - 11)
            when_live(finish, k - 12)
            if vector_takes_both:
                when_live(scale_shift_1, k - 6, 0, True)
            if vector_shares:
                when_live(scale_shift_1, k - 6, 1, True)
            when_live(group_h, k - 8)
            if not vector_normalises:
                when_live(normalise_1, k - 4, False)
            when_live(gelu, k - 1)
            when_live(var_1, k - 3, k)
            when_live(var_2, k - 11, k)
            inv_std(k, k - 3, k - 11)
            if not vector_takes_both:
                when_live(scale_shift_1, k - 6, 0, False)
            when_live(mean_2, k - 10)
            if not vector_shares:
                when_live(scale_shift_1, k - 6, 1, False)
            when_live(moments_1, k - 2)
            when_live(mean_1, k - 1)
            when_live(moments_2, k - 10)
            when_live(quantise_h, k - 8)
            if vector_normalises:
                when_live(normalise_1, k - 4, True)
            when_live(transpose_n, k - 5)
            if k != -1:
                when_live(quantise_z, k + 2)
